import numpy as np
import ml_dtypes


def mxq(x, axis, fmt="e4m3"):
    dtype, down = {"e4m3": (ml_dtypes.float8_e4m3fn, 7), "e5m2": (ml_dtypes.float8_e5m2, 14)}[fmt]
    v = np.moveaxis(np.asarray(x, np.float32).astype(ml_dtypes.bfloat16).astype(np.float64), axis, -1)
    blocks = v.reshape(v.shape[:-1] + (-1, 32))
    amax = np.abs(blocks).max(-1, keepdims=True)
    byte = np.maximum(np.where(amax > 0, np.frexp(amax)[1] - 1 + 127, 0) - down, 1)
    scale = np.exp2(byte - 127.0)
    codes = (blocks / scale).astype(np.float32).astype(dtype).astype(np.float64)
    return np.moveaxis((codes * scale).reshape(v.shape), -1, axis)


WIDE = False


def mx_kscale(k):
    if not WIDE:
        return np.ones(k)
    levels = np.array([10, -10, 5, -5, 0])
    if k % 512:
        return np.exp2(np.random.permutation(np.resize(levels, k // 32))).repeat(32)
    a = np.empty((k // 512, 16))
    for p in range(k // 512):
        a[p, :8] = np.random.permutation(np.resize(levels, 8))
        for g in range(8):
            far = levels[np.abs(levels - a[p, g]) >= 10]
            a[p, g + 8] = far[np.random.randint(len(far))]
    return np.exp2(a.ravel()).repeat(32)


BF16 = ml_dtypes.bfloat16


def bf(x):
    return np.asarray(x, np.float32).astype(BF16)


def f64(x):
    return np.asarray(x).astype(np.float64)


L, P, B, H = 4, 1, 2048, 1024
KEEP_PROB = 0.7


def preact(h_in, w, masks, mu, sigma, z):
    wm = f64(w)[0] * f64(masks)[0]
    noise = np.exp(f64(mu)[0][None, :] + f64(sigma)[0][None, :] * f64(z)[0])
    return f64(h_in) @ wm.T + noise


def setup_inputs():
    s = mx_kscale(B)[:, None]
    u = mx_kscale(H)
    w0 = bf(np.random.standard_normal((P, H, H)) / np.sqrt(H))
    h0 = bf(np.random.standard_normal((B, H)) * 1.3)
    masks = bf(np.random.uniform(size=(P, H, H)) < KEEP_PROB)
    mu = bf(np.random.uniform(-0.5, 0.5, (P, H)))
    sigma = bf(np.random.uniform(0.05, 0.5, (P, H)))
    z = bf(np.random.standard_normal((P, B, H)))
    g = np.random.standard_normal((B, H)) * np.exp2(np.random.randint(-6, 1, (B, 1))) * 2.0
    pre = preact(h0, w0, masks, mu, sigma, z)
    return {"h_in": bf(f64(h0) * s),
            "w": bf(f64(w0) / u[None, :, None]),
            "masks": masks,
            "mu": mu,
            "sigma": sigma,
            "z": z,
            "pre": np.asarray(pre, np.float32),
            "grad_out": bf(g / s * u[None, :])}


def reference(h_in, w, masks, mu, sigma, z, pre, grad_out):
    m = f64(masks)[0]
    wm = f64(w)[0] * m
    dz = np.where(f64(pre) > 0.0, f64(grad_out), 0.0)
    dh = mxq(dz, 1, "e5m2") @ mxq(wm, 0, "e4m3")
    dwm = mxq(dz, 0, "e5m2").T @ mxq(f64(h_in), 0, "e4m3")
    dw = (dwm * m)[None, :, :]
    return dh, dw

@@ -1,0 +1,335 @@
+from contextlib import ExitStack
+
+import concourse.mybir as mybir
+from concourse.masks import make_identity
+
+TOKENS, FEATS, INS = 2048, 1024, 1024
+FLOPS = 4 * TOKENS * FEATS * INS
+BYTES = 2 * TOKENS * INS + 4 * FEATS * INS + 6 * TOKENS * FEATS + 4 * TOKENS * INS + 4 * FEATS * INS
+
+F32 = mybir.dt.float32
+BF16 = mybir.dt.bfloat16
+U32 = mybir.dt.uint32
+U8 = mybir.dt.uint8
+E4M3 = mybir.dt.float8_e4m3fn_x4
+E5M2 = mybir.dt.float8_e5m2_x4
+MUL = mybir.AluOpType.mult
+GT = mybir.AluOpType.is_gt
+
+P = 128
+J = 4
+GROUPS = TOKENS // 512
+HALF = 512
+STEPS = ((0, 0), (0, 1), (1, 0), (1, 1), (2, 0), (3, 0), (2, 1), (3, 1))
+
+
+def tile_scm_mlp_pa_v_kernel(tc, h_in, w, masks, mu, sigma, z, pre, grad_out, out_0, out_1):
+    nc = tc.nc
+    pre_v = pre.rearrange("(g p j) w -> g p j w", p=P, j=J)
+    grad_v = grad_out.rearrange("(g p j) w -> g p j w", p=P, j=J)
+    h_v = h_in.rearrange("(g p j) i -> g p j i", p=P, j=J)
+    w_v = w[0, :, :].rearrange("(f q t) i -> f q t i", q=P, t=J)
+    m_v = masks[0, :, :].rearrange("(f q t) i -> f q t i", q=P, t=J)
+    dx_v = out_0.rearrange("(g p j) i -> g p j i", p=P, j=J)
+    dw_v = out_1[0, :, :].rearrange("(f q t) i -> f q t i", q=P, t=J)
+
+    with ExitStack() as ctx:
+        keep = ctx.enter_context(tc.tile_pool(name="keep", bufs=1))
+        pool = ctx.enter_context(tc.tile_pool(name="pool", bufs=2))
+        psum = ctx.enter_context(tc.psum_pool(name="psum", bufs=1))
+
+        ident = keep.tile([P, P], F32, name="ident")
+        make_identity(nc, ident[:])
+        ident_b = keep.tile([P, P], BF16, name="ident_b")
+        nc.vector.tensor_copy(out=ident_b[:], in_=ident[:])
+
+        zt_c = keep.tile([P, GROUPS, FEATS], U32, align_bytes=64, name="zt_c")
+        zt_s = keep.tile([P, GROUPS, FEATS], U8, align_bytes=64, name="zt_s")
+        zf_c = keep.tile([P, GROUPS, 2, HALF], U32, align_bytes=64, name="zf_c")
+        zf_s = keep.tile([P, GROUPS, 2, HALF], U8, align_bytes=64, name="zf_s")
+        h_c = keep.tile([P, GROUPS, INS], U32, align_bytes=64, name="h_c")
+        h_s = keep.tile([P, GROUPS, INS], U8, align_bytes=64, name="h_s")
+        w_c = keep.tile([P, 2, INS], U32, align_bytes=64, name="w_c")
+        w_s = keep.tile([P, 2, INS], U8, align_bytes=64, name="w_s")
+        mask = keep.tile([P, 2, J, INS], BF16, align_bytes=64, name="mask")
+
+        pre_t, grad_t, h_t, w_t = {}, {}, {}, {}
+        dz_t, zi_t, zf_t, hi_t, wi_t = {}, {}, {}, {}, {}
+        acc = {}
+
+        def load_step(s, parts=1):
+            g, f = STEPS[s]
+            cols = slice(f * HALF, (f + 1) * HALF)
+            a = pool.tile([P, J, HALF], F32, tag="pre", bufs=3, name="pre_tile")
+            b = pool.tile([P, J, HALF], BF16, tag="grad", bufs=3, name="grad_tile")
+            for k in range(parts):
+                js = slice(k * J // parts, (k + 1) * J // parts)
+                nc.sync.dma_start(out=a[:, js, :], in_=pre_v[g, :, js, cols])
+                nc.sync.dma_start(out=b[:, js, :], in_=grad_v[g, :, js, cols])
+            pre_t[s], grad_t[s] = a, b
+
+        def load_h(g):
+            a = pool.tile([P, J, INS], BF16, tag="wh", bufs=4, name="h_tile")
+            nc.sync.dma_start(out=a[:], in_=h_v[g, :, :, :])
+            h_t[g] = a
+
+        def load_w(f):
+            nc.sync.dma_start(out=mask[:, f, :, :], in_=m_v[f, :, :, :])
+            a = pool.tile([P, J, INS], BF16, tag="wh", bufs=4, name="w_tile")
+            nc.sync.dma_start(out=a[:], in_=w_v[f, :, :, :])
+            w_t[f] = a
+
+        def gate(s, parts=1):
+            a = pool.tile([P, J, HALF], BF16, tag="dz", bufs=3, align_bytes=64, name="dz_tile")
+            for k in range(parts):
+                js = slice(k * J // parts, (k + 1) * J // parts)
+                nc.vector.scalar_tensor_tensor(
+                    out=a[:, js, :], in0=pre_t[s][:, js, :], scalar=0.0, in1=grad_t[s][:, js, :], op0=GT, op1=MUL
+                )
+            dz_t[s] = a
+
+        def turn(s):
+            words = dz_t[s][:].rearrange("p j w -> p (j w)").bitcast(F32)
+            b = pool.tile([P, J, P, J], BF16, tag="zf", bufs=2, align_bytes=64, name="zf_tile")
+            zf_t[s] = b
+            bw = b[:].rearrange("q j p t -> q (j p t)").bitcast(F32).rearrange("q (j p u) -> q j p u", j=J, u=2)
+            for half in range(2):
+                a = psum.tile([P, 2, 2, P], F32, tag="turn", bufs=2, name="turn_ps")
+                for jj in range(2):
+                    for u in range(2):
+                        first = (2 * half + jj) * (HALF // 2) + u
+                        nc.tensor.transpose(a[:, jj, u, :], words[:, first : first + HALF // 2 - 1 : 2], ident[:])
+                nc.scalar.copy(out=bw[:, 2 * half : 2 * half + 2, :, :], in_=a[:].rearrange("q j u p -> q j p u"))
+
+        def spread(s, engine="v"):
+            a = pool.tile([P, J, P, J], BF16, tag="zi", bufs=2, align_bytes=64, name="zi_tile")
+            src = dz_t[s][:].rearrange("p j (q t) -> p t q j", t=J)
+            if engine == "v":
+                nc.vector.tensor_copy(out=a[:], in_=src)
+            else:
+                nc.scalar.copy(out=a[:], in_=src)
+            zi_t[s] = a
+
+        def q_tok(s):
+            g, f = STEPS[s]
+            cols = slice(f * HALF, (f + 1) * HALF)
+            nc.vector.quantize_mx(
+                out=zt_c[:, g, cols].bitcast(E5M2), scales=zt_s[:, g, cols], in_=zi_t[s][:].rearrange("p t q j -> p (t q j)")
+            )
+
+        def q_feat(s):
+            g, f = STEPS[s]
+            nc.vector.quantize_mx(
+                out=zf_c[:, g, f, :].bitcast(E5M2), scales=zf_s[:, g, f, :], in_=zf_t[s][:].rearrange("q j p t -> q (j p t)")
+            )
+
+        def interleave(engine, src):
+            a = pool.tile([P, HALF, J], BF16, tag="mix", bufs=3, align_bytes=64, name="mix_tile")
+            dst = a[:].rearrange("p (c i) t -> p c t i", i=4)
+            view = src.rearrange("p t (c i) -> p c t i", i=4)
+            if engine == "s":
+                nc.scalar.copy(out=dst, in_=view)
+            else:
+                nc.vector.tensor_copy(out=dst, in_=view)
+            return a
+
+        def h_spread(g, n):
+            hi_t[g, n] = interleave("s", h_t[g][:, :, n * HALF : (n + 1) * HALF])
+
+        def h_turn(g, n):
+            a = pool.tile([P, HALF, J], BF16, tag="mix", bufs=3, align_bytes=64, name="mix_tile")
+            for q in range(2):
+                first = n * HALF + q * 256
+                b = psum.tile([P, 256, J], BF16, tag="turn", bufs=2, name="h_ps")
+                for r in range(2):
+                    cols = slice(first + r * P, first + (r + 1) * P)
+                    nc.tensor.matmul(
+                        out=b[:, r * P : (r + 1) * P, :],
+                        lhsT=ident_b[:],
+                        rhs=h_t[g][:, :, cols].rearrange("p j i -> p i j"),
+                        start=True,
+                        stop=True,
+                    )
+                nc.scalar.copy(out=a[:, q * 256 : (q + 1) * 256, :], in_=b[:])
+            hi_t[g, n] = a
+
+        def q_h(g, n):
+            cols = slice(n * HALF, (n + 1) * HALF)
+            nc.vector.quantize_mx(
+                out=h_c[:, g, cols].bitcast(E4M3), scales=h_s[:, g, cols], in_=hi_t[g, n][:].rearrange("p i t -> p (i t)")
+            )
+
+        def w_mask(f):
+            nc.vector.tensor_tensor(out=w_t[f][:], in0=w_t[f][:], in1=mask[:, f, :, :], op=MUL)
+
+        def w_spread(f, n):
+            wi_t[f, n] = interleave("s", w_t[f][:, :, n * HALF : (n + 1) * HALF])
+
+        def q_w(f, n):
+            cols = slice(n * HALF, (n + 1) * HALF)
+            nc.vector.quantize_mx(
+                out=w_c[:, f, cols].bitcast(E4M3), scales=w_s[:, f, cols], in_=wi_t[f, n][:].rearrange("p i t -> p (i t)")
+            )
+
+        def dx(g, j, where):
+            o = pool.tile([P, INS], F32, tag="ost", bufs=6, name="dx_tile")
+            for n in range(2):
+                a = psum.tile([P, HALF], F32, tag="x", bufs=2, name="dx_ps")
+                for f in range(2):
+                    nc.tensor.matmul_mx(
+                        out=a[:],
+                        lhsT=zf_c[:, g, f, j * P : (j + 1) * P].bitcast(E5M2),
+                        lhsT_scale=zf_s[:, g, f, j * P : (j + 1) * P],
+                        rhs=w_c[:, f, n * HALF : (n + 1) * HALF].bitcast(E4M3),
+                        rhs_scale=w_s[:, f, n * HALF : (n + 1) * HALF],
+                        start=(f == 0),
+                        stop=(f == 1),
+                    )
+                if where[n] == "s":
+                    nc.scalar.copy(out=o[:, n * HALF : (n + 1) * HALF], in_=a[:])
+                else:
+                    nc.vector.tensor_copy(out=o[:, n * HALF : (n + 1) * HALF], in_=a[:])
+            nc.sync.dma_start(out=dx_v[g, :, j, :], in_=o[:])
+
+        def dw_pass(f, n, g, ts=range(J), tags=("acc",) * J):
+            for t in ts:
+                if g == 0:
+                    acc[t] = psum.tile([P, HALF], F32, tag=tags[t], bufs=4 if tags[t] == "acc" else 2, name="dw_ps")
+                cols = slice(f * HALF + t * P, f * HALF + (t + 1) * P)
+                nc.tensor.matmul_mx(
+                    out=acc[t][:],
+                    lhsT=zt_c[:, g, cols].bitcast(E5M2),
+                    lhsT_scale=zt_s[:, g, cols],
+                    rhs=h_c[:, g, n * HALF : (n + 1) * HALF].bitcast(E4M3),
+                    rhs_scale=h_s[:, g, n * HALF : (n + 1) * HALF],
+                    start=(g == 0),
+                    stop=(g == GROUPS - 1),
+                )
+
+        def dw_out(f, n, t):
+            cols = slice(n * HALF, (n + 1) * HALF)
+            o = pool.tile([P, HALF], F32, tag="wst", bufs=4, name="dw_tile")
+            nc.vector.tensor_tensor(out=o[:], in0=acc[t][:], in1=mask[:, f, t, cols], op=MUL)
+            nc.sync.dma_start(out=dw_v[f, :, t, cols], in_=o[:])
+
+        with tc.manual_schedule():
+            load_step(0, 2)
+            load_w(0)
+            load_step(1)
+            load_w(1)
+            load_step(2)
+            load_h(0)
+            load_h(1)
+
+            gate(0, 2)
+            turn(0)
+            spread(0)
+            w_mask(0)
+            w_spread(0, 0)
+            w_spread(0, 1)
+            load_step(3)
+
+            gate(1)
+            turn(1)
+            q_tok(0)
+            q_feat(0)
+            spread(1)
+            w_mask(1)
+            w_spread(1, 0)
+            q_w(0, 0)
+            q_w(0, 1)
+            w_spread(1, 1)
+            load_step(4)
+            load_h(2)
+
+            gate(2)
+            turn(2)
+            q_tok(1)
+            q_feat(1)
+            h_turn(0, 0)
+            spread(2)
+            q_w(1, 0)
+            q_w(1, 1)
+            h_turn(0, 1)
+            dx(0, 0, "ss")
+            dx(0, 1, "ss")
+            load_step(5)
+            load_h(3)
+
+            gate(3)
+            turn(3)
+            q_tok(2)
+            q_feat(2)
+            h_turn(1, 0)
+            spread(3)
+            q_h(0, 0)
+            q_h(0, 1)
+            h_turn(1, 1)
+            dx(0, 2, "ss")
+            dx(0, 3, "ss")
+            dw_pass(0, 0, 0)
+            load_step(6)
+
+            gate(4)
+            turn(4)
+            q_tok(3)
+            q_feat(3)
+            h_spread(2, 0)
+            spread(4)
+            q_h(1, 0)
+            q_h(1, 1)
+            dx(1, 0, "ss")
+            dx(1, 1, "ss")
+            dw_pass(0, 0, 1)
+            load_step(7)
+
+            gate(5)
+            turn(5)
+            q_tok(4)
+            q_feat(4)
+            h_spread(2, 1)
+            spread(5)
+            q_h(2, 0)
+            h_turn(3, 0)
+            dx(1, 2, "ss")
+            dx(1, 3, "ss")
+
+            gate(6)
+            turn(6)
+            q_tok(5)
+            q_feat(5)
+            h_turn(3, 1)
+            spread(6)
+            q_h(2, 1)
+            dw_pass(0, 0, 2)
+            q_h(3, 0)
+            dw_pass(0, 0, 3)
+
+            gate(7)
+            turn(7)
+            q_feat(6)
+            q_tok(6)
+            for t in range(4):
+                dw_out(0, 0, t)
+            q_h(3, 1)
+            spread(7)
+            dx(2, 0, "ss")
+            for t in range(4):
+                for g in range(4):
+                    dw_pass(0, 1, g, (t,))
+                if t % 2:
+                    dx(2, 1 + t // 2, "ss")
+            q_feat(7)
+            q_tok(7)
+            for t in range(4):
+                dw_out(0, 1, t)
+            dx(2, 3, "ss")
+            for t in range(4):
+                dx(3, t, "ss")
+                for g in range(4):
+                    dw_pass(1, 0, g, (t,))
+                dw_out(1, 0, t)
+            for t in range(4):
+                for g in range(4):
+                    dw_pass(1, 1, g, (t,))
+                dw_out(1, 1, t)

@@ -73,10 +73,12 @@ def tile_scm_mlp_pa_v_kernel(tc, h_in, w, masks, mu, sigma, z, pre, grad_out, ou
             nc.sync.dma_start(out=a[:], in_=h_v[g, :, :, :])
             h_t[g] = a
 
-        def load_w(f):
-            nc.sync.dma_start(out=mask[:, f, :, :], in_=m_v[f, :, :, :])
+        def load_w(f, parts=1):
             a = pool.tile([P, J, INS], BF16, tag="wh", bufs=4, name="w_tile")
-            nc.sync.dma_start(out=a[:], in_=w_v[f, :, :, :])
+            for k in range(parts):
+                cols = slice(k * INS // parts, (k + 1) * INS // parts)
+                nc.sync.dma_start(out=a[:, :, cols], in_=w_v[f, :, :, cols])
+                nc.sync.dma_start(out=mask[:, f, :, cols], in_=m_v[f, :, :, cols])
             w_t[f] = a
 
         def gate(s, parts=1):
@@ -159,8 +161,9 @@ def tile_scm_mlp_pa_v_kernel(tc, h_in, w, masks, mu, sigma, z, pre, grad_out, ou
                 out=h_c[:, g, cols].bitcast(E4M3), scales=h_s[:, g, cols], in_=hi_t[g, n][:].rearrange("p i t -> p (i t)")
             )
 
-        def w_mask(f):
-            nc.vector.tensor_tensor(out=w_t[f][:], in0=w_t[f][:], in1=mask[:, f, :, :], op=MUL)
+        def w_mask(f, n):
+            cols = slice(n * HALF, (n + 1) * HALF)
+            nc.vector.tensor_tensor(out=w_t[f][:, :, cols], in0=w_t[f][:, :, cols], in1=mask[:, f, :, cols], op=MUL)
 
         def w_spread(f, n):
             wi_t[f, n] = interleave("s", w_t[f][:, :, n * HALF : (n + 1) * HALF])
@@ -213,31 +216,34 @@ def tile_scm_mlp_pa_v_kernel(tc, h_in, w, masks, mu, sigma, z, pre, grad_out, ou
             nc.sync.dma_start(out=dw_v[f, :, t, cols], in_=o[:])
 
         with tc.manual_schedule():
-            load_step(0, 2)
-            load_w(0)
+            load_w(0, 2)
+            load_step(0)
             load_step(1)
+            load_h(0)
             load_w(1)
             load_step(2)
-            load_h(0)
             load_h(1)
 
-            gate(0, 2)
+            w_mask(0, 0)
+            w_spread(0, 0)
+            w_mask(0, 1)
+            w_spread(0, 1)
+            gate(0)
             turn(0)
             spread(0)
-            w_mask(0)
-            w_spread(0, 0)
-            w_spread(0, 1)
+            q_w(0, 0)
             load_step(3)
 
             gate(1)
             turn(1)
+            h_spread(0, 0)
+            q_w(0, 1)
             q_tok(0)
             q_feat(0)
             spread(1)
-            w_mask(1)
+            w_mask(1, 0)
             w_spread(1, 0)
-            q_w(0, 0)
-            q_w(0, 1)
+            w_mask(1, 1)
             w_spread(1, 1)
             load_step(4)
             load_h(2)
@@ -246,89 +252,88 @@ def tile_scm_mlp_pa_v_kernel(tc, h_in, w, masks, mu, sigma, z, pre, grad_out, ou
             turn(2)
             q_tok(1)
             q_feat(1)
-            h_turn(0, 0)
             spread(2)
+            q_h(0, 0)
             q_w(1, 0)
-            q_w(1, 1)
-            h_turn(0, 1)
-            dx(0, 0, "ss")
-            dx(0, 1, "ss")
             load_step(5)
-            load_h(3)
+            h_spread(0, 1)
 
             gate(3)
             turn(3)
+            q_w(1, 1)
             q_tok(2)
             q_feat(2)
-            h_turn(1, 0)
+            dx(0, 0, "ss")
+            dx(0, 1, "ss")
+            h_spread(1, 0)
             spread(3)
-            q_h(0, 0)
             q_h(0, 1)
-            h_turn(1, 1)
-            dx(0, 2, "ss")
-            dx(0, 3, "ss")
-            dw_pass(0, 0, 0)
             load_step(6)
+            load_h(3)
 
             gate(4)
             turn(4)
             q_tok(3)
             q_feat(3)
+            dx(0, 2, "ss")
+            dx(0, 3, "ss")
             h_spread(2, 0)
+            dw_pass(0, 0, 0)
             spread(4)
             q_h(1, 0)
-            q_h(1, 1)
-            dx(1, 0, "ss")
-            dx(1, 1, "ss")
-            dw_pass(0, 0, 1)
             load_step(7)
 
             gate(5)
             turn(5)
             q_tok(4)
             q_feat(4)
-            h_spread(2, 1)
-            spread(5)
+            dx(1, 0, "ss")
+            h_spread(3, 0)
+            dx(1, 1, "ss")
+            dw_pass(0, 0, 1)
             q_h(2, 0)
-            h_turn(3, 0)
-            dx(1, 2, "ss")
-            dx(1, 3, "ss")
+            spread(5)
 
             gate(6)
             turn(6)
+            h_spread(1, 1)
             q_tok(5)
             q_feat(5)
-            h_turn(3, 1)
             spread(6)
-            q_h(2, 1)
-            dw_pass(0, 0, 2)
             q_h(3, 0)
+            dx(1, 2, "ss")
+            dw_pass(0, 0, 2)
+            dx(1, 3, "ss")
             dw_pass(0, 0, 3)
 
             gate(7)
             turn(7)
+            h_spread(2, 1)
             q_feat(6)
             q_tok(6)
+            q_h(1, 1)
             for t in range(4):
                 dw_out(0, 0, t)
-            q_h(3, 1)
+            q_h(2, 1)
             spread(7)
             dx(2, 0, "ss")
-            for t in range(4):
-                for g in range(4):
-                    dw_pass(0, 1, g, (t,))
-                if t % 2:
-                    dx(2, 1 + t // 2, "ss")
+            for g in range(3):
+                dw_pass(1, 0, g)
+            h_spread(3, 1)
+            dx(2, 1, "ss")
             q_feat(7)
             q_tok(7)
-            for t in range(4):
-                dw_out(0, 1, t)
+            q_h(3, 1)
+            dx(2, 2, "ss")
+            dw_pass(1, 0, 3)
             dx(2, 3, "ss")
+            for t in range(4):
+                dw_out(1, 0, t)
             for t in range(4):
                 dx(3, t, "ss")
                 for g in range(4):
-                    dw_pass(1, 0, g, (t,))
-                dw_out(1, 0, t)
+                    dw_pass(0, 1, g, (t,))
+                dw_out(0, 1, t)
             for t in range(4):
                 for g in range(4):
                     dw_pass(1, 1, g, (t,))

@@ -20,7 +20,6 @@ P = 128
 J = 4
 GROUPS = TOKENS // 512
 HALF = 512
-STEPS = ((0, 0), (0, 1), (1, 0), (1, 1), (2, 0), (3, 0), (2, 1), (3, 1))
 
 
 def tile_scm_mlp_pa_v_kernel(tc, h_in, w, masks, mu, sigma, z, pre, grad_out, out_0, out_1):
@@ -36,17 +35,13 @@ def tile_scm_mlp_pa_v_kernel(tc, h_in, w, masks, mu, sigma, z, pre, grad_out, ou
     with ExitStack() as ctx:
         keep = ctx.enter_context(tc.tile_pool(name="keep", bufs=1))
         pool = ctx.enter_context(tc.tile_pool(name="pool", bufs=2))
-        psum = ctx.enter_context(tc.psum_pool(name="psum", bufs=1))
+        psum = ctx.enter_context(tc.psum_pool(name="psum", bufs=2))
 
         ident = keep.tile([P, P], F32, name="ident")
         make_identity(nc, ident[:])
-        ident_b = keep.tile([P, P], BF16, name="ident_b")
-        nc.vector.tensor_copy(out=ident_b[:], in_=ident[:])
 
         zt_c = keep.tile([P, GROUPS, FEATS], U32, align_bytes=64, name="zt_c")
         zt_s = keep.tile([P, GROUPS, FEATS], U8, align_bytes=64, name="zt_s")
-        zf_c = keep.tile([P, GROUPS, 2, HALF], U32, align_bytes=64, name="zf_c")
-        zf_s = keep.tile([P, GROUPS, 2, HALF], U8, align_bytes=64, name="zf_s")
         h_c = keep.tile([P, GROUPS, INS], U32, align_bytes=64, name="h_c")
         h_s = keep.tile([P, GROUPS, INS], U8, align_bytes=64, name="h_s")
         w_c = keep.tile([P, 2, INS], U32, align_bytes=64, name="w_c")
@@ -55,286 +50,316 @@ def tile_scm_mlp_pa_v_kernel(tc, h_in, w, masks, mu, sigma, z, pre, grad_out, ou
 
         pre_t, grad_t, h_t, w_t = {}, {}, {}, {}
         dz_t, zi_t, zf_t, hi_t, wi_t = {}, {}, {}, {}, {}
-        acc = {}
+        acc, dx_t, zf_c, zf_s = {}, {}, {}, {}
 
-        def load_step(s, parts=1):
-            g, f = STEPS[s]
-            cols = slice(f * HALF, (f + 1) * HALF)
-            a = pool.tile([P, J, HALF], F32, tag="pre", bufs=3, name="pre_tile")
-            b = pool.tile([P, J, HALF], BF16, tag="grad", bufs=3, name="grad_tile")
-            for k in range(parts):
-                js = slice(k * J // parts, (k + 1) * J // parts)
-                nc.sync.dma_start(out=a[:, js, :], in_=pre_v[g, :, js, cols])
-                nc.sync.dma_start(out=b[:, js, :], in_=grad_v[g, :, js, cols])
-            pre_t[s], grad_t[s] = a, b
+        def half(n):
+            return slice(n * HALF, (n + 1) * HALF)
+
+        def move(engine, out, in_):
+            if engine == "s":
+                nc.scalar.copy(out=out, in_=in_)
+            else:
+                nc.vector.tensor_copy(out=out, in_=in_)
+
+        def load_pre(g, f=None):
+            if f != 1:
+                a = pool.tile([P, J, FEATS], F32, tag="pre", name="pre_tile")
+                pre_t[g] = a
+            cols = slice(0, FEATS) if f is None else half(f)
+            nc.sync.dma_start(out=pre_t[g][:, :, cols], in_=pre_v[g, :, :, cols])
+
+        def load_grad(g, f=None):
+            if f != 1:
+                a = pool.tile([P, J, FEATS], BF16, tag="grad", name="grad_tile")
+                grad_t[g] = a
+            cols = slice(0, FEATS) if f is None else half(f)
+            nc.sync.dma_start(out=grad_t[g][:, :, cols], in_=grad_v[g, :, :, cols])
 
         def load_h(g):
-            a = pool.tile([P, J, INS], BF16, tag="wh", bufs=4, name="h_tile")
+            a = pool.tile([P, J, INS], BF16, tag="wh", bufs=3, name="h_tile")
             nc.sync.dma_start(out=a[:], in_=h_v[g, :, :, :])
             h_t[g] = a
 
-        def load_w(f, parts=1):
-            a = pool.tile([P, J, INS], BF16, tag="wh", bufs=4, name="w_tile")
-            for k in range(parts):
-                cols = slice(k * INS // parts, (k + 1) * INS // parts)
-                nc.sync.dma_start(out=a[:, :, cols], in_=w_v[f, :, :, cols])
-                nc.sync.dma_start(out=mask[:, f, :, cols], in_=m_v[f, :, :, cols])
-            w_t[f] = a
+        def load_w(f, n=None):
+            if n != 1:
+                a = pool.tile([P, J, INS], BF16, tag="wh", bufs=3, name="w_tile")
+                w_t[f] = a
+            cols = slice(0, INS) if n is None else half(n)
+            nc.sync.dma_start(out=w_t[f][:, :, cols], in_=w_v[f, :, :, cols])
 
-        def gate(s, parts=1):
-            a = pool.tile([P, J, HALF], BF16, tag="dz", bufs=3, align_bytes=64, name="dz_tile")
-            for k in range(parts):
-                js = slice(k * J // parts, (k + 1) * J // parts)
-                nc.vector.scalar_tensor_tensor(
-                    out=a[:, js, :], in0=pre_t[s][:, js, :], scalar=0.0, in1=grad_t[s][:, js, :], op0=GT, op1=MUL
-                )
-            dz_t[s] = a
+        def load_mask(f, n=None):
+            cols = slice(0, INS) if n is None else half(n)
+            nc.sync.dma_start(out=mask[:, f, :, cols], in_=m_v[f, :, :, cols])
 
-        def turn(s):
-            words = dz_t[s][:].rearrange("p j w -> p (j w)").bitcast(F32)
-            b = pool.tile([P, J, P, J], BF16, tag="zf", bufs=2, align_bytes=64, name="zf_tile")
-            zf_t[s] = b
+        def gate(g, f):
+            a = pool.tile([P, J, HALF], BF16, tag="dz", bufs=5, align_bytes=64, name="dz_tile")
+            nc.vector.scalar_tensor_tensor(
+                out=a[:], in0=pre_t[g][:, :, half(f)], scalar=0.0, in1=grad_t[g][:, :, half(f)], op0=GT, op1=MUL
+            )
+            dz_t[g, f] = a
+
+        def turn(g, f):
+            words = dz_t[g, f][:].rearrange("p j w -> p (j w)").bitcast(F32)
+            b = pool.tile([P, J, P, J], BF16, tag="zf", align_bytes=64, name="zf_tile")
+            zf_t[g, f] = b
             bw = b[:].rearrange("q j p t -> q (j p t)").bitcast(F32).rearrange("q (j p u) -> q j p u", j=J, u=2)
-            for half in range(2):
-                a = psum.tile([P, 2, 2, P], F32, tag="turn", bufs=2, name="turn_ps")
+            for k in range(2):
+                a = psum.tile([P, 2, 2, P], F32, tag="turn", name="turn_ps")
                 for jj in range(2):
                     for u in range(2):
-                        first = (2 * half + jj) * (HALF // 2) + u
+                        first = (2 * k + jj) * (HALF // 2) + u
                         nc.tensor.transpose(a[:, jj, u, :], words[:, first : first + HALF // 2 - 1 : 2], ident[:])
-                nc.scalar.copy(out=bw[:, 2 * half : 2 * half + 2, :, :], in_=a[:].rearrange("q j u p -> q j p u"))
+                nc.scalar.copy(out=bw[:, 2 * k : 2 * k + 2, :, :], in_=a[:].rearrange("q j u p -> q j p u"))
 
-        def spread(s, engine="v"):
-            a = pool.tile([P, J, P, J], BF16, tag="zi", bufs=2, align_bytes=64, name="zi_tile")
-            src = dz_t[s][:].rearrange("p j (q t) -> p t q j", t=J)
-            if engine == "v":
-                nc.vector.tensor_copy(out=a[:], in_=src)
-            else:
-                nc.scalar.copy(out=a[:], in_=src)
-            zi_t[s] = a
+        def spread_dz(g, f, engine="v"):
+            a = pool.tile([P, J, P, J], BF16, tag="zi", align_bytes=64, name="zi_tile")
+            move(engine, a[:], dz_t[g, f][:].rearrange("p j (q t) -> p t q j", t=J))
+            zi_t[g, f] = a
 
-        def q_tok(s):
-            g, f = STEPS[s]
-            cols = slice(f * HALF, (f + 1) * HALF)
+        def quant_tok(g, f):
             nc.vector.quantize_mx(
-                out=zt_c[:, g, cols].bitcast(E5M2), scales=zt_s[:, g, cols], in_=zi_t[s][:].rearrange("p t q j -> p (t q j)")
+                out=zt_c[:, g, half(f)].bitcast(E5M2),
+                scales=zt_s[:, g, half(f)],
+                in_=zi_t[g, f][:].rearrange("p t q j -> p (t q j)"),
             )
 
-        def q_feat(s):
-            g, f = STEPS[s]
+        def quant_feat(g, f):
+            if f == 0:
+                a = pool.tile([P, 2, HALF], U32, tag="zfc", align_bytes=64, name="zf_codes")
+                b = pool.tile([P, 2, HALF], U8, tag="zfs", align_bytes=64, name="zf_scales")
+                zf_c[g], zf_s[g] = a, b
             nc.vector.quantize_mx(
-                out=zf_c[:, g, f, :].bitcast(E5M2), scales=zf_s[:, g, f, :], in_=zf_t[s][:].rearrange("q j p t -> q (j p t)")
+                out=zf_c[g][:, f, :].bitcast(E5M2),
+                scales=zf_s[g][:, f, :],
+                in_=zf_t[g, f][:].rearrange("q j p t -> q (j p t)"),
             )
 
         def interleave(engine, src):
             a = pool.tile([P, HALF, J], BF16, tag="mix", bufs=3, align_bytes=64, name="mix_tile")
-            dst = a[:].rearrange("p (c i) t -> p c t i", i=4)
-            view = src.rearrange("p t (c i) -> p c t i", i=4)
-            if engine == "s":
-                nc.scalar.copy(out=dst, in_=view)
-            else:
-                nc.vector.tensor_copy(out=dst, in_=view)
+            move(engine, a[:].rearrange("p (c i) t -> p c t i", i=4), src.rearrange("p t (c i) -> p c t i", i=4))
             return a
 
-        def h_spread(g, n):
-            hi_t[g, n] = interleave("s", h_t[g][:, :, n * HALF : (n + 1) * HALF])
+        def spread_h(g, n, engine="s"):
+            hi_t[g, n] = interleave(engine, h_t[g][:, :, half(n)])
 
-        def h_turn(g, n):
-            a = pool.tile([P, HALF, J], BF16, tag="mix", bufs=3, align_bytes=64, name="mix_tile")
-            for q in range(2):
-                first = n * HALF + q * 256
-                b = psum.tile([P, 256, J], BF16, tag="turn", bufs=2, name="h_ps")
-                for r in range(2):
-                    cols = slice(first + r * P, first + (r + 1) * P)
-                    nc.tensor.matmul(
-                        out=b[:, r * P : (r + 1) * P, :],
-                        lhsT=ident_b[:],
-                        rhs=h_t[g][:, :, cols].rearrange("p j i -> p i j"),
-                        start=True,
-                        stop=True,
-                    )
-                nc.scalar.copy(out=a[:, q * 256 : (q + 1) * 256, :], in_=b[:])
-            hi_t[g, n] = a
-
-        def q_h(g, n):
-            cols = slice(n * HALF, (n + 1) * HALF)
+        def quant_h(g, n):
             nc.vector.quantize_mx(
-                out=h_c[:, g, cols].bitcast(E4M3), scales=h_s[:, g, cols], in_=hi_t[g, n][:].rearrange("p i t -> p (i t)")
+                out=h_c[:, g, half(n)].bitcast(E4M3),
+                scales=h_s[:, g, half(n)],
+                in_=hi_t[g, n][:].rearrange("p i t -> p (i t)"),
             )
 
-        def w_mask(f, n):
-            cols = slice(n * HALF, (n + 1) * HALF)
-            nc.vector.tensor_tensor(out=w_t[f][:, :, cols], in0=w_t[f][:, :, cols], in1=mask[:, f, :, cols], op=MUL)
-
-        def w_spread(f, n):
-            wi_t[f, n] = interleave("s", w_t[f][:, :, n * HALF : (n + 1) * HALF])
-
-        def q_w(f, n):
-            cols = slice(n * HALF, (n + 1) * HALF)
-            nc.vector.quantize_mx(
-                out=w_c[:, f, cols].bitcast(E4M3), scales=w_s[:, f, cols], in_=wi_t[f, n][:].rearrange("p i t -> p (i t)")
+        def mask_w(f, n):
+            nc.vector.tensor_tensor(
+                out=w_t[f][:, :, half(n)], in0=w_t[f][:, :, half(n)], in1=mask[:, f, :, half(n)], op=MUL
             )
 
-        def dx(g, j, where):
-            o = pool.tile([P, INS], F32, tag="ost", bufs=6, name="dx_tile")
+        def spread_w(f, n, engine="s"):
+            wi_t[f, n] = interleave(engine, w_t[f][:, :, half(n)])
+
+        def quant_w(f, n):
+            nc.vector.quantize_mx(
+                out=w_c[:, f, half(n)].bitcast(E4M3),
+                scales=w_s[:, f, half(n)],
+                in_=wi_t[f, n][:].rearrange("p i t -> p (i t)"),
+            )
+
+        def dx(g, j, engines="ss"):
+            if j % 2 == 0:
+                o = pool.tile([P, 2, INS], F32, tag="ost", bufs=4, name="dx_tile")
+                dx_t[g, j // 2] = o
+            banks = []
             for n in range(2):
-                a = psum.tile([P, HALF], F32, tag="x", bufs=2, name="dx_ps")
+                a = psum.tile([P, HALF], F32, tag="x", name="dx_ps")
                 for f in range(2):
                     nc.tensor.matmul_mx(
                         out=a[:],
-                        lhsT=zf_c[:, g, f, j * P : (j + 1) * P].bitcast(E5M2),
-                        lhsT_scale=zf_s[:, g, f, j * P : (j + 1) * P],
-                        rhs=w_c[:, f, n * HALF : (n + 1) * HALF].bitcast(E4M3),
-                        rhs_scale=w_s[:, f, n * HALF : (n + 1) * HALF],
+                        lhsT=zf_c[g][:, f, j * P : (j + 1) * P].bitcast(E5M2),
+                        lhsT_scale=zf_s[g][:, f, j * P : (j + 1) * P],
+                        rhs=w_c[:, f, half(n)].bitcast(E4M3),
+                        rhs_scale=w_s[:, f, half(n)],
                         start=(f == 0),
                         stop=(f == 1),
                     )
-                if where[n] == "s":
-                    nc.scalar.copy(out=o[:, n * HALF : (n + 1) * HALF], in_=a[:])
-                else:
-                    nc.vector.tensor_copy(out=o[:, n * HALF : (n + 1) * HALF], in_=a[:])
-            nc.sync.dma_start(out=dx_v[g, :, j, :], in_=o[:])
+                banks.append(a)
+            for n in range(2):
+                move(engines[n], dx_t[g, j // 2][:, j % 2, half(n)], banks[n][:])
 
-        def dw_pass(f, n, g, ts=range(J), tags=("acc",) * J):
-            for t in ts:
+        def store_dx(g, k):
+            nc.sync.dma_start(out=dx_v[g, :, 2 * k : 2 * k + 2, :], in_=dx_t[g, k][:])
+
+        def dw(f, t, g):
+            for n in range(2):
                 if g == 0:
-                    acc[t] = psum.tile([P, HALF], F32, tag=tags[t], bufs=4 if tags[t] == "acc" else 2, name="dw_ps")
+                    a = psum.tile([P, HALF], F32, tag="acc" + str(n), name="dw_ps")
+                    acc[f, t, n] = a
                 cols = slice(f * HALF + t * P, f * HALF + (t + 1) * P)
                 nc.tensor.matmul_mx(
-                    out=acc[t][:],
+                    out=acc[f, t, n][:],
                     lhsT=zt_c[:, g, cols].bitcast(E5M2),
                     lhsT_scale=zt_s[:, g, cols],
-                    rhs=h_c[:, g, n * HALF : (n + 1) * HALF].bitcast(E4M3),
-                    rhs_scale=h_s[:, g, n * HALF : (n + 1) * HALF],
+                    rhs=h_c[:, g, half(n)].bitcast(E4M3),
+                    rhs_scale=h_s[:, g, half(n)],
                     start=(g == 0),
                     stop=(g == GROUPS - 1),
                 )
 
-        def dw_out(f, n, t):
-            cols = slice(n * HALF, (n + 1) * HALF)
-            o = pool.tile([P, HALF], F32, tag="wst", bufs=4, name="dw_tile")
-            nc.vector.tensor_tensor(out=o[:], in0=acc[t][:], in1=mask[:, f, t, cols], op=MUL)
-            nc.sync.dma_start(out=dw_v[f, :, t, cols], in_=o[:])
+        def out_dw(f, t):
+            o = pool.tile([P, INS], F32, tag="ost", bufs=4, name="dw_tile")
+            for n in range(2):
+                nc.vector.tensor_tensor(out=o[:, half(n)], in0=acc[f, t, n][:], in1=mask[:, f, t, half(n)], op=MUL)
+            nc.sync.dma_start(out=dw_v[f, :, t, :], in_=o[:])
 
         with tc.manual_schedule():
-            load_w(0, 2)
-            load_step(0)
-            load_step(1)
-            load_h(0)
-            load_w(1)
-            load_step(2)
+            load_mask(1)
             load_h(1)
-
-            w_mask(0, 0)
-            w_spread(0, 0)
-            w_mask(0, 1)
-            w_spread(0, 1)
-            gate(0)
-            turn(0)
-            spread(0)
-            q_w(0, 0)
-            load_step(3)
-
-            gate(1)
-            turn(1)
-            h_spread(0, 0)
-            q_w(0, 1)
-            q_tok(0)
-            q_feat(0)
-            spread(1)
-            w_mask(1, 0)
-            w_spread(1, 0)
-            w_mask(1, 1)
-            w_spread(1, 1)
-            load_step(4)
+            load_pre(0, 0)
+            load_grad(0, 0)
+            spread_h(1, 1)
+            load_w(1)
+            gate(0, 0)
+            quant_h(1, 1)
+            load_w(0, 0)
+            mask_w(1, 0)
+            load_mask(0, 0)
+            spread_h(1, 0)
+            load_grad(0, 1)
+            mask_w(1, 1)
+            quant_h(1, 0)
+            spread_dz(0, 0, "s")
+            mask_w(0, 0)
+            spread_w(0, 0, "v")
+            load_pre(0, 1)
+            gate(0, 1)
+            quant_w(0, 0)
+            spread_w(1, 1)
+            load_mask(0, 1)
+            load_w(0, 1)
+            turn(0, 0)
+            load_grad(1)
+            quant_feat(0, 0)
+            spread_w(1, 0)
+            quant_tok(0, 0)
+            spread_dz(0, 1, "s")
+            load_pre(1)
+            quant_w(1, 1)
+            mask_w(0, 1)
+            quant_w(1, 0)
+            turn(0, 1)
+            quant_tok(0, 1)
+            load_h(0)
             load_h(2)
-
-            gate(2)
-            turn(2)
-            q_tok(1)
-            q_feat(1)
-            spread(2)
-            q_h(0, 0)
-            q_w(1, 0)
-            load_step(5)
-            h_spread(0, 1)
-
-            gate(3)
-            turn(3)
-            q_w(1, 1)
-            q_tok(2)
-            q_feat(2)
-            dx(0, 0, "ss")
-            dx(0, 1, "ss")
-            h_spread(1, 0)
-            spread(3)
-            q_h(0, 1)
-            load_step(6)
+            load_pre(2)
+            quant_feat(0, 1)
+            spread_w(0, 1)
+            load_grad(2)
+            quant_w(0, 1)
+            dx(0, 0)
+            dx(0, 2)
+            spread_h(0, 0)
+            gate(1, 0)
+            gate(1, 1)
+            load_grad(3)
             load_h(3)
-
-            gate(4)
-            turn(4)
-            q_tok(3)
-            q_feat(3)
-            dx(0, 2, "ss")
-            dx(0, 3, "ss")
-            h_spread(2, 0)
-            dw_pass(0, 0, 0)
-            spread(4)
-            q_h(1, 0)
-            load_step(7)
-
-            gate(5)
-            turn(5)
-            q_tok(4)
-            q_feat(4)
-            dx(1, 0, "ss")
-            h_spread(3, 0)
-            dx(1, 1, "ss")
-            dw_pass(0, 0, 1)
-            q_h(2, 0)
-            spread(5)
-
-            gate(6)
-            turn(6)
-            h_spread(1, 1)
-            q_tok(5)
-            q_feat(5)
-            spread(6)
-            q_h(3, 0)
-            dx(1, 2, "ss")
-            dw_pass(0, 0, 2)
-            dx(1, 3, "ss")
-            dw_pass(0, 0, 3)
-
-            gate(7)
-            turn(7)
-            h_spread(2, 1)
-            q_feat(6)
-            q_tok(6)
-            q_h(1, 1)
-            for t in range(4):
-                dw_out(0, 0, t)
-            q_h(2, 1)
-            spread(7)
-            dx(2, 0, "ss")
-            for g in range(3):
-                dw_pass(1, 0, g)
-            h_spread(3, 1)
-            dx(2, 1, "ss")
-            q_feat(7)
-            q_tok(7)
-            q_h(3, 1)
-            dx(2, 2, "ss")
-            dw_pass(1, 0, 3)
-            dx(2, 3, "ss")
-            for t in range(4):
-                dw_out(1, 0, t)
-            for t in range(4):
-                dx(3, t, "ss")
-                for g in range(4):
-                    dw_pass(0, 1, g, (t,))
-                dw_out(0, 1, t)
-            for t in range(4):
-                for g in range(4):
-                    dw_pass(1, 1, g, (t,))
-                dw_out(1, 1, t)
+            turn(1, 0)
+            spread_h(0, 1, "v")
+            quant_feat(1, 0)
+            quant_h(0, 0)
+            dx(0, 3)
+            spread_h(2, 0, "v")
+            turn(1, 1)
+            quant_h(0, 1)
+            quant_feat(1, 1)
+            dx(0, 1)
+            spread_dz(1, 0, "s")
+            load_pre(3)
+            dw(0, 1, 0)
+            spread_h(2, 1, "v")
+            gate(2, 0)
+            store_dx(0, 0)
+            quant_tok(1, 0)
+            dx(1, 2)
+            dw(0, 0, 0)
+            dx(1, 0)
+            spread_dz(2, 0, "s")
+            quant_h(2, 0)
+            gate(2, 1)
+            quant_h(2, 1)
+            turn(2, 0)
+            quant_feat(2, 0)
+            spread_h(3, 1, "v")
+            dw(0, 1, 1)
+            quant_tok(2, 0)
+            dx(1, 1)
+            store_dx(0, 1)
+            turn(2, 1)
+            quant_feat(2, 1)
+            dw(0, 0, 1)
+            dx(1, 3)
+            dw(0, 1, 2)
+            spread_h(3, 0)
+            store_dx(1, 0)
+            dx(2, 0)
+            gate(3, 0)
+            gate(3, 1)
+            dw(0, 0, 2)
+            turn(3, 0)
+            dx(2, 1)
+            turn(3, 1)
+            spread_dz(3, 0)
+            quant_h(3, 0)
+            quant_tok(3, 0)
+            store_dx(1, 1)
+            quant_h(3, 1)
+            dx(2, 2, "sv")
+            dw(0, 1, 3)
+            store_dx(2, 0)
+            out_dw(0, 1)
+            dw(0, 0, 3)
+            spread_dz(1, 1, "s")
+            dx(2, 3)
+            quant_feat(3, 0)
+            store_dx(2, 1)
+            out_dw(0, 0)
+            dw(0, 3, 0)
+            dw(0, 3, 1)
+            quant_tok(1, 1)
+            quant_feat(3, 1)
+            dw(0, 3, 2)
+            dw(0, 3, 3)
+            spread_dz(2, 1, "s")
+            dw(0, 2, 0)
+            dw(0, 2, 1)
+            out_dw(0, 3)
+            spread_dz(3, 1, "s")
+            dx(3, 0, "sv")
+            dw(0, 2, 2)
+            dw(0, 2, 3)
+            dw(1, 0, 0)
+            quant_tok(3, 1)
+            dw(1, 0, 1)
+            out_dw(0, 2)
+            dx(3, 1, "vv")
+            dw(1, 1, 0)
+            quant_tok(2, 1)
+            dx(3, 2, "vv")
+            dw(1, 0, 2)
+            dx(3, 3, "vv")
+            store_dx(3, 0)
+            dw(1, 0, 3)
+            dw(1, 1, 1)
+            store_dx(3, 1)
+            dw(1, 1, 2)
+            dw(1, 1, 3)
+            out_dw(1, 0)
+            dw(1, 2, 0)
+            dw(1, 2, 1)
+            dw(1, 2, 2)
+            dw(1, 2, 3)
+            out_dw(1, 1)
+            dw(1, 3, 0)
+            out_dw(1, 2)
+            dw(1, 3, 1)
+            dw(1, 3, 2)
+            dw(1, 3, 3)
+            out_dw(1, 3)

@@ -113,7 +113,7 @@ def tile_scm_mlp_pa_v_kernel(tc, h_in, w, masks, mu, sigma, z, pre, grad_out, ou
 
         def spread_dz(g, f, engine="v"):
             a = pool.tile([P, J, P, J], BF16, tag="zi", align_bytes=64, name="zi_tile")
-            move(engine, a[:], dz_t[g, f][:].rearrange("p j (q t) -> p t q j", t=J))
+            move(engine, a[:].rearrange("p t q j -> p q t j"), dz_t[g, f][:].rearrange("p j (q t) -> p q t j", t=J))
             zi_t[g, f] = a
 
         def quant_tok(g, f):
@@ -124,7 +124,7 @@ def tile_scm_mlp_pa_v_kernel(tc, h_in, w, masks, mu, sigma, z, pre, grad_out, ou
             )
 
         def quant_feat(g, f):
-            if f == 0:
+            if g not in zf_c:
                 a = pool.tile([P, 2, HALF], U32, tag="zfc", align_bytes=64, name="zf_codes")
                 b = pool.tile([P, 2, HALF], U8, tag="zfs", align_bytes=64, name="zf_scales")
                 zf_c[g], zf_s[g] = a, b
@@ -211,155 +211,153 @@ def tile_scm_mlp_pa_v_kernel(tc, h_in, w, masks, mu, sigma, z, pre, grad_out, ou
             nc.sync.dma_start(out=dw_v[f, :, t, :], in_=o[:])
 
         with tc.manual_schedule():
-            load_mask(1)
-            load_h(1)
-            load_pre(0, 0)
             load_grad(0, 0)
-            spread_h(1, 1)
+            load_mask(1)
+            load_pre(0, 0)
             load_w(1)
             gate(0, 0)
-            quant_h(1, 1)
-            load_w(0, 0)
-            mask_w(1, 0)
-            load_mask(0, 0)
-            spread_h(1, 0)
+            load_mask(0)
+            load_w(0)
             load_grad(0, 1)
             mask_w(1, 1)
-            quant_h(1, 0)
-            spread_dz(0, 0, "s")
-            mask_w(0, 0)
-            spread_w(0, 0, "v")
-            load_pre(0, 1)
-            gate(0, 1)
-            quant_w(0, 0)
+            mask_w(1, 0)
             spread_w(1, 1)
-            load_mask(0, 1)
-            load_w(0, 1)
-            turn(0, 0)
-            load_grad(1)
-            quant_feat(0, 0)
+            spread_dz(0, 0)
             spread_w(1, 0)
-            quant_tok(0, 0)
-            spread_dz(0, 1, "s")
-            load_pre(1)
+            load_pre(0, 1)
             quant_w(1, 1)
             mask_w(0, 1)
-            quant_w(1, 0)
-            turn(0, 1)
-            quant_tok(0, 1)
+            turn(0, 0)
+            mask_w(0, 0)
             load_h(0)
-            load_h(2)
+            spread_w(0, 1)
+            quant_w(1, 0)
+            quant_tok(0, 0)
+            quant_feat(0, 0)
+            spread_w(0, 0)
+            gate(0, 1)
+            spread_dz(0, 1)
+            load_pre(1)
+            load_grad(1)
+            load_h(1)
+            turn(0, 1)
+            quant_w(0, 1)
+            load_grad(2)
             load_pre(2)
             quant_feat(0, 1)
-            spread_w(0, 1)
-            load_grad(2)
-            quant_w(0, 1)
-            dx(0, 0)
-            dx(0, 2)
+            quant_tok(0, 1)
+            quant_w(0, 0)
+            spread_h(0, 1)
+            dx(0, 0, "vv")
             spread_h(0, 0)
+            load_h(2)
+            quant_h(0, 0)
             gate(1, 0)
+            dx(0, 2)
+            dx(0, 1)
+            dx(0, 3)
             gate(1, 1)
-            load_grad(3)
             load_h(3)
             turn(1, 0)
-            spread_h(0, 1, "v")
-            quant_feat(1, 0)
-            quant_h(0, 0)
-            dx(0, 3)
-            spread_h(2, 0, "v")
-            turn(1, 1)
             quant_h(0, 1)
-            quant_feat(1, 1)
-            dx(0, 1)
-            spread_dz(1, 0, "s")
             load_pre(3)
-            dw(0, 1, 0)
-            spread_h(2, 1, "v")
-            gate(2, 0)
-            store_dx(0, 0)
-            quant_tok(1, 0)
-            dx(1, 2)
-            dw(0, 0, 0)
+            turn(1, 1)
+            quant_feat(1, 0)
+            spread_h(1, 0)
+            spread_dz(1, 0)
+            quant_feat(1, 1)
             dx(1, 0)
-            spread_dz(2, 0, "s")
-            quant_h(2, 0)
-            gate(2, 1)
-            quant_h(2, 1)
-            turn(2, 0)
-            quant_feat(2, 0)
-            spread_h(3, 1, "v")
-            dw(0, 1, 1)
-            quant_tok(2, 0)
+            quant_tok(1, 0)
+            load_grad(3)
             dx(1, 1)
-            store_dx(0, 1)
+            spread_h(1, 1, "v")
+            gate(2, 1)
+            gate(2, 0)
+            dx(1, 2)
+            quant_h(1, 1)
             turn(2, 1)
+            spread_dz(2, 0)
+            dw(0, 0, 0)
+            quant_h(1, 0)
+            spread_h(2, 1)
+            turn(2, 0)
             quant_feat(2, 1)
+            spread_h(2, 0)
+            spread_dz(2, 1)
+            quant_h(2, 1)
             dw(0, 0, 1)
-            dx(1, 3)
-            dw(0, 1, 2)
+            store_dx(0, 0)
+            quant_tok(2, 0)
+            dw(0, 1, 0)
             spread_h(3, 0)
-            store_dx(1, 0)
+            dx(1, 3, "vs")
+            dw(0, 1, 1)
+            quant_h(2, 0)
+            quant_feat(2, 0)
+            spread_h(3, 1)
             dx(2, 0)
             gate(3, 0)
             gate(3, 1)
             dw(0, 0, 2)
+            store_dx(0, 1)
+            dw(0, 1, 2)
+            spread_dz(3, 0)
             turn(3, 0)
             dx(2, 1)
             turn(3, 1)
-            spread_dz(3, 0)
             quant_h(3, 0)
             quant_tok(3, 0)
-            store_dx(1, 1)
+            dx(2, 2)
             quant_h(3, 1)
-            dx(2, 2, "sv")
-            dw(0, 1, 3)
-            store_dx(2, 0)
-            out_dw(0, 1)
+            store_dx(1, 0)
             dw(0, 0, 3)
-            spread_dz(1, 1, "s")
+            dw(0, 1, 3)
             dx(2, 3)
-            quant_feat(3, 0)
+            store_dx(1, 1)
+            store_dx(2, 0)
             store_dx(2, 1)
+            quant_feat(3, 1)
             out_dw(0, 0)
             dw(0, 3, 0)
+            out_dw(0, 1)
             dw(0, 3, 1)
-            quant_tok(1, 1)
-            quant_feat(3, 1)
             dw(0, 3, 2)
-            dw(0, 3, 3)
-            spread_dz(2, 1, "s")
+            quant_feat(3, 0)
             dw(0, 2, 0)
+            quant_tok(2, 1)
+            spread_dz(1, 1)
+            dw(0, 3, 3)
             dw(0, 2, 1)
-            out_dw(0, 3)
-            spread_dz(3, 1, "s")
-            dx(3, 0, "sv")
             dw(0, 2, 2)
             dw(0, 2, 3)
-            dw(1, 0, 0)
-            quant_tok(3, 1)
-            dw(1, 0, 1)
+            out_dw(0, 3)
+            quant_tok(1, 1)
             out_dw(0, 2)
-            dx(3, 1, "vv")
+            dx(3, 2)
+            spread_dz(3, 1)
             dw(1, 1, 0)
-            quant_tok(2, 1)
-            dx(3, 2, "vv")
-            dw(1, 0, 2)
-            dx(3, 3, "vv")
-            store_dx(3, 0)
-            dw(1, 0, 3)
+            quant_tok(3, 1)
             dw(1, 1, 1)
-            store_dx(3, 1)
             dw(1, 1, 2)
+            dw(1, 0, 0)
+            dx(3, 3, "sv")
+            store_dx(3, 1)
+            dw(1, 0, 1)
             dw(1, 1, 3)
+            out_dw(1, 1)
+            dx(3, 0, "vv")
+            dw(1, 0, 2)
+            dw(1, 0, 3)
             out_dw(1, 0)
             dw(1, 2, 0)
+            dx(3, 1, "vv")
             dw(1, 2, 1)
-            dw(1, 2, 2)
-            dw(1, 2, 3)
-            out_dw(1, 1)
             dw(1, 3, 0)
-            out_dw(1, 2)
+            dw(1, 2, 2)
+            store_dx(3, 0)
+            dw(1, 2, 3)
             dw(1, 3, 1)
             dw(1, 3, 2)
             dw(1, 3, 3)
+            out_dw(1, 2)
             out_dw(1, 3)

@@ -4,8 +4,8 @@ import concourse.mybir as mybir
 from concourse.masks import make_identity
 
 TOKENS, FEATS, INS = 2048, 1024, 1024
-FLOPS = 4 * TOKENS * FEATS * INS
-BYTES = 2 * TOKENS * INS + 4 * FEATS * INS + 6 * TOKENS * FEATS + 4 * TOKENS * INS + 4 * FEATS * INS
+FLOPS = 2 * (2 * TOKENS * FEATS * INS)
+BYTES = 2 * (TOKENS * INS + 2 * FEATS * INS + TOKENS * FEATS) + 4 * (TOKENS * FEATS + TOKENS * INS + FEATS * INS)
 
 F32 = mybir.dt.float32
 BF16 = mybir.dt.bfloat16
@@ -13,24 +13,29 @@ U32 = mybir.dt.uint32
 U8 = mybir.dt.uint8
 E4M3 = mybir.dt.float8_e4m3fn_x4
 E5M2 = mybir.dt.float8_e5m2_x4
-MUL = mybir.AluOpType.mult
-GT = mybir.AluOpType.is_gt
+MULT = mybir.AluOpType.mult
+IS_GT = mybir.AluOpType.is_gt
 
 P = 128
-J = 4
-GROUPS = TOKENS // 512
-HALF = 512
+PACK = 4
+HALF = P * PACK
+GROUPS = TOKENS // HALF
+
+IN_TURN_BANKS = ((1, 1), (1, 2))
 
 
 def tile_scm_mlp_pa_v_kernel(tc, h_in, w, masks, mu, sigma, z, pre, grad_out, out_0, out_1):
     nc = tc.nc
-    pre_v = pre.rearrange("(g p j) w -> g p j w", p=P, j=J)
-    grad_v = grad_out.rearrange("(g p j) w -> g p j w", p=P, j=J)
-    h_v = h_in.rearrange("(g p j) i -> g p j i", p=P, j=J)
-    w_v = w[0, :, :].rearrange("(f q t) i -> f q t i", q=P, t=J)
-    m_v = masks[0, :, :].rearrange("(f q t) i -> f q t i", q=P, t=J)
-    dx_v = out_0.rearrange("(g p j) i -> g p j i", p=P, j=J)
-    dw_v = out_1[0, :, :].rearrange("(f q t) i -> f q t i", q=P, t=J)
+    pre_v = pre.rearrange("(g p j) w -> g p j w", p=P, j=PACK)
+    grad_v = grad_out.rearrange("(g p j) w -> g p j w", p=P, j=PACK)
+    h_v = h_in.rearrange("(g p j) i -> g p j i", p=P, j=PACK)
+    w_v = w[0, :, :].rearrange("(f q t) i -> f q t i", q=P, t=PACK)
+    mask_v = masks[0, :, :].rearrange("(f q t) i -> f q t i", q=P, t=PACK)
+    dx_v = out_0.rearrange("(g p j) i -> g p j i", p=P, j=PACK)
+    dw_v = out_1[0, :, :].rearrange("(f q t) i -> f q t i", q=P, t=PACK)
+
+    def half(n):
+        return slice(n * HALF, (n + 1) * HALF)
 
     with ExitStack() as ctx:
         keep = ctx.enter_context(tc.tile_pool(name="keep", bufs=1))
@@ -40,20 +45,18 @@ def tile_scm_mlp_pa_v_kernel(tc, h_in, w, masks, mu, sigma, z, pre, grad_out, ou
         ident = keep.tile([P, P], F32, name="ident")
         make_identity(nc, ident[:])
 
-        zt_c = keep.tile([P, GROUPS, FEATS], U32, align_bytes=64, name="zt_c")
-        zt_s = keep.tile([P, GROUPS, FEATS], U8, align_bytes=64, name="zt_s")
-        h_c = keep.tile([P, GROUPS, INS], U32, align_bytes=64, name="h_c")
-        h_s = keep.tile([P, GROUPS, INS], U8, align_bytes=64, name="h_s")
-        w_c = keep.tile([P, 2, INS], U32, align_bytes=64, name="w_c")
-        w_s = keep.tile([P, 2, INS], U8, align_bytes=64, name="w_s")
-        mask = keep.tile([P, 2, J, INS], BF16, align_bytes=64, name="mask")
+        z_tok_codes = keep.tile([P, GROUPS, FEATS], U32, align_bytes=64, name="z_tok_codes")
+        z_tok_scales = keep.tile([P, GROUPS, FEATS], U8, align_bytes=64, name="z_tok_scales")
+        h_codes = keep.tile([P, GROUPS, INS], U32, align_bytes=64, name="h_codes")
+        h_scales = keep.tile([P, GROUPS, INS], U8, align_bytes=64, name="h_scales")
+        w_codes = keep.tile([P, 2, INS], U32, align_bytes=64, name="w_codes")
+        w_scales = keep.tile([P, 2, INS], U8, align_bytes=64, name="w_scales")
+        mask = keep.tile([P, 2, PACK, INS], BF16, align_bytes=64, name="mask")
 
-        pre_t, grad_t, h_t, w_t = {}, {}, {}, {}
-        dz_t, zi_t, zf_t, hi_t, wi_t = {}, {}, {}, {}, {}
-        acc, dx_t, zf_c, zf_s = {}, {}, {}, {}
-
-        def half(n):
-            return slice(n * HALF, (n + 1) * HALF)
+        pre_t, grad_t, h_t, w_t, dz_t = {}, {}, {}, {}, {}
+        dz_tok_by4, dz_feat_by4, h_by4, w_by4 = {}, {}, {}, {}
+        z_feat_codes, z_feat_scales = {}, {}
+        dx_t, dw_acc = {}, {}
 
         def move(engine, out, in_):
             if engine == "s":
@@ -61,303 +64,314 @@ def tile_scm_mlp_pa_v_kernel(tc, h_in, w, masks, mu, sigma, z, pre, grad_out, ou
             else:
                 nc.vector.tensor_copy(out=out, in_=in_)
 
-        def load_pre(g, f=None):
-            if f != 1:
-                a = pool.tile([P, J, FEATS], F32, tag="pre", name="pre_tile")
-                pre_t[g] = a
-            cols = slice(0, FEATS) if f is None else half(f)
-            nc.sync.dma_start(out=pre_t[g][:, :, cols], in_=pre_v[g, :, :, cols])
+        def load_step_part(src, tiles, dtype, tag, g, cols, rows):
+            if g not in tiles:
+                new = pool.tile([P, PACK, FEATS], dtype, tag=tag, name="group_tile")
+                tiles[g] = new
+            nc.sync.dma_start(out=tiles[g][:, rows, cols], in_=src[g, :, rows, cols])
 
-        def load_grad(g, f=None):
-            if f != 1:
-                a = pool.tile([P, J, FEATS], BF16, tag="grad", name="grad_tile")
-                grad_t[g] = a
-            cols = slice(0, FEATS) if f is None else half(f)
-            nc.sync.dma_start(out=grad_t[g][:, :, cols], in_=grad_v[g, :, :, cols])
+        def load_pre(g, cols=slice(0, FEATS), rows=slice(0, PACK)):
+            load_step_part(pre_v, pre_t, F32, "pre", g, cols, rows)
+
+        def load_grad(g, cols=slice(0, FEATS), rows=slice(0, PACK)):
+            load_step_part(grad_v, grad_t, BF16, "grad", g, cols, rows)
 
         def load_h(g):
-            a = pool.tile([P, J, INS], BF16, tag="wh", bufs=3, name="h_tile")
-            nc.sync.dma_start(out=a[:], in_=h_v[g, :, :, :])
-            h_t[g] = a
+            new = pool.tile([P, PACK, INS], BF16, tag="h_or_w", bufs=3, name="h_tile")
+            nc.sync.dma_start(out=new[:], in_=h_v[g, :, :, :])
+            h_t[g] = new
 
-        def load_w(f, n=None):
-            if n != 1:
-                a = pool.tile([P, J, INS], BF16, tag="wh", bufs=3, name="w_tile")
-                w_t[f] = a
-            cols = slice(0, INS) if n is None else half(n)
-            nc.sync.dma_start(out=w_t[f][:, :, cols], in_=w_v[f, :, :, cols])
+        def load_w(f):
+            new = pool.tile([P, PACK, INS], BF16, tag="h_or_w", bufs=3, name="w_tile")
+            nc.sync.dma_start(out=new[:], in_=w_v[f, :, :, :])
+            w_t[f] = new
 
-        def load_mask(f, n=None):
-            cols = slice(0, INS) if n is None else half(n)
-            nc.sync.dma_start(out=mask[:, f, :, cols], in_=m_v[f, :, :, cols])
+        def load_mask(f):
+            nc.sync.dma_start(out=mask[:, f, :, :], in_=mask_v[f, :, :, :])
 
-        def gate(g, f):
-            a = pool.tile([P, J, HALF], BF16, tag="dz", bufs=5, align_bytes=64, name="dz_tile")
+        def gate(g, f, rows=slice(0, PACK)):
+            if (g, f) not in dz_t:
+                new = pool.tile([P, PACK, HALF], BF16, tag="dz", bufs=5, align_bytes=64, name="dz_tile")
+                dz_t[g, f] = new
             nc.vector.scalar_tensor_tensor(
-                out=a[:], in0=pre_t[g][:, :, half(f)], scalar=0.0, in1=grad_t[g][:, :, half(f)], op0=GT, op1=MUL
+                out=dz_t[g, f][:, rows, :],
+                in0=pre_t[g][:, rows, half(f)],
+                scalar=0.0,
+                in1=grad_t[g][:, rows, half(f)],
+                op0=IS_GT,
+                op1=MULT,
             )
-            dz_t[g, f] = a
 
         def turn(g, f):
             words = dz_t[g, f][:].rearrange("p j w -> p (j w)").bitcast(F32)
-            b = pool.tile([P, J, P, J], BF16, tag="zf", align_bytes=64, name="zf_tile")
-            zf_t[g, f] = b
-            bw = b[:].rearrange("q j p t -> q (j p t)").bitcast(F32).rearrange("q (j p u) -> q j p u", j=J, u=2)
-            for k in range(2):
-                a = psum.tile([P, 2, 2, P], F32, tag="turn", name="turn_ps")
-                for jj in range(2):
+            new = pool.tile([P, PACK, P, PACK], BF16, tag="dz_feat_by4", align_bytes=64, name="feat_tile")
+            dz_feat_by4[g, f] = new
+            new_words = new[:].rearrange("q j p t -> q (j p t)").bitcast(F32)
+            new_words = new_words.rearrange("q (j p u) -> q j p u", j=PACK, u=2)
+            for pair in range(2):
+                bank = psum.tile([P, 2, 2, P], F32, tag="turn", name="turn_bank")
+                for k in range(2):
                     for u in range(2):
-                        first = (2 * k + jj) * (HALF // 2) + u
-                        nc.tensor.transpose(a[:, jj, u, :], words[:, first : first + HALF // 2 - 1 : 2], ident[:])
-                nc.scalar.copy(out=bw[:, 2 * k : 2 * k + 2, :, :], in_=a[:].rearrange("q j u p -> q j p u"))
+                        first = (2 * pair + k) * (HALF // 2) + u
+                        nc.tensor.transpose(bank[:, k, u, :], words[:, first : first + HALF // 2 - 1 : 2], ident[:])
+                nc.scalar.copy(
+                    out=new_words[:, 2 * pair : 2 * pair + 2, :, :], in_=bank[:].rearrange("q k u p -> q k p u")
+                )
 
-        def spread_dz(g, f, engine="v"):
-            a = pool.tile([P, J, P, J], BF16, tag="zi", align_bytes=64, name="zi_tile")
-            move(engine, a[:].rearrange("p t q j -> p q t j"), dz_t[g, f][:].rearrange("p j (q t) -> p q t j", t=J))
-            zi_t[g, f] = a
+        def quant_feat(g, f):
+            if g not in z_feat_codes:
+                codes = pool.tile([P, 2, HALF], U32, tag="z_feat_codes", align_bytes=64, name="feat_codes")
+                scales = pool.tile([P, 2, HALF], U8, tag="z_feat_scales", align_bytes=64, name="feat_scales")
+                z_feat_codes[g], z_feat_scales[g] = codes, scales
+            nc.vector.quantize_mx(
+                out=z_feat_codes[g][:, f, :].bitcast(E5M2),
+                scales=z_feat_scales[g][:, f, :],
+                in_=dz_feat_by4[g, f][:].rearrange("q j p t -> q (j p t)"),
+            )
+
+        def spread_dz(g, f):
+            new = pool.tile([P, PACK, P, PACK], BF16, tag="dz_tok_by4", align_bytes=64, name="tok_tile")
+            nc.vector.tensor_copy(
+                out=new[:].rearrange("p t q j -> p q t j"),
+                in_=dz_t[g, f][:].rearrange("p j (q t) -> p q t j", t=PACK),
+            )
+            dz_tok_by4[g, f] = new
 
         def quant_tok(g, f):
             nc.vector.quantize_mx(
-                out=zt_c[:, g, half(f)].bitcast(E5M2),
-                scales=zt_s[:, g, half(f)],
-                in_=zi_t[g, f][:].rearrange("p t q j -> p (t q j)"),
+                out=z_tok_codes[:, g, half(f)].bitcast(E5M2),
+                scales=z_tok_scales[:, g, half(f)],
+                in_=dz_tok_by4[g, f][:].rearrange("p t q j -> p (t q j)"),
             )
 
-        def quant_feat(g, f):
-            if g not in zf_c:
-                a = pool.tile([P, 2, HALF], U32, tag="zfc", align_bytes=64, name="zf_codes")
-                b = pool.tile([P, 2, HALF], U8, tag="zfs", align_bytes=64, name="zf_scales")
-                zf_c[g], zf_s[g] = a, b
-            nc.vector.quantize_mx(
-                out=zf_c[g][:, f, :].bitcast(E5M2),
-                scales=zf_s[g][:, f, :],
-                in_=zf_t[g, f][:].rearrange("q j p t -> q (j p t)"),
-            )
-
-        def interleave(engine, src):
-            a = pool.tile([P, HALF, J], BF16, tag="mix", bufs=3, align_bytes=64, name="mix_tile")
-            move(engine, a[:].rearrange("p (c i) t -> p c t i", i=4), src.rearrange("p t (c i) -> p c t i", i=4))
-            return a
+        def by4(engine, src):
+            new = pool.tile([P, HALF, PACK], BF16, tag="by4", bufs=3, align_bytes=64, name="by4_tile")
+            move(engine, new[:].rearrange("p (c i) t -> p c t i", i=4), src.rearrange("p t (c i) -> p c t i", i=4))
+            return new
 
         def spread_h(g, n, engine="s"):
-            hi_t[g, n] = interleave(engine, h_t[g][:, :, half(n)])
+            h_by4[g, n] = by4(engine, h_t[g][:, :, half(n)])
 
         def quant_h(g, n):
             nc.vector.quantize_mx(
-                out=h_c[:, g, half(n)].bitcast(E4M3),
-                scales=h_s[:, g, half(n)],
-                in_=hi_t[g, n][:].rearrange("p i t -> p (i t)"),
+                out=h_codes[:, g, half(n)].bitcast(E4M3),
+                scales=h_scales[:, g, half(n)],
+                in_=h_by4[g, n][:].rearrange("p i j -> p (i j)"),
             )
 
         def mask_w(f, n):
             nc.vector.tensor_tensor(
-                out=w_t[f][:, :, half(n)], in0=w_t[f][:, :, half(n)], in1=mask[:, f, :, half(n)], op=MUL
+                out=w_t[f][:, :, half(n)], in0=w_t[f][:, :, half(n)], in1=mask[:, f, :, half(n)], op=MULT
             )
 
         def spread_w(f, n, engine="s"):
-            wi_t[f, n] = interleave(engine, w_t[f][:, :, half(n)])
+            w_by4[f, n] = by4(engine, w_t[f][:, :, half(n)])
 
         def quant_w(f, n):
             nc.vector.quantize_mx(
-                out=w_c[:, f, half(n)].bitcast(E4M3),
-                scales=w_s[:, f, half(n)],
-                in_=wi_t[f, n][:].rearrange("p i t -> p (i t)"),
+                out=w_codes[:, f, half(n)].bitcast(E4M3),
+                scales=w_scales[:, f, half(n)],
+                in_=w_by4[f, n][:].rearrange("q i t -> q (i t)"),
             )
 
         def dx(g, j, engines="ss"):
-            if j % 2 == 0:
-                o = pool.tile([P, 2, INS], F32, tag="ost", bufs=4, name="dx_tile")
-                dx_t[g, j // 2] = o
+            pair, k = divmod(j, 2)
+            if (g, pair) not in dx_t:
+                new = pool.tile([P, 2, INS], F32, tag="result", bufs=4, name="dx_tile")
+                dx_t[g, pair] = new
+            cols = slice(j * P, (j + 1) * P)
             banks = []
             for n in range(2):
-                a = psum.tile([P, HALF], F32, tag="x", name="dx_ps")
+                bank = psum.tile([P, HALF], F32, tag="dx", name="dx_bank")
                 for f in range(2):
                     nc.tensor.matmul_mx(
-                        out=a[:],
-                        lhsT=zf_c[g][:, f, j * P : (j + 1) * P].bitcast(E5M2),
-                        lhsT_scale=zf_s[g][:, f, j * P : (j + 1) * P],
-                        rhs=w_c[:, f, half(n)].bitcast(E4M3),
-                        rhs_scale=w_s[:, f, half(n)],
+                        out=bank[:],
+                        lhsT=z_feat_codes[g][:, f, cols].bitcast(E5M2),
+                        lhsT_scale=z_feat_scales[g][:, f, cols],
+                        rhs=w_codes[:, f, half(n)].bitcast(E4M3),
+                        rhs_scale=w_scales[:, f, half(n)],
                         start=(f == 0),
                         stop=(f == 1),
                     )
-                banks.append(a)
+                banks.append(bank)
             for n in range(2):
-                move(engines[n], dx_t[g, j // 2][:, j % 2, half(n)], banks[n][:])
+                move(engines[n], dx_t[g, pair][:, k, half(n)], banks[n][:])
 
-        def store_dx(g, k):
-            nc.sync.dma_start(out=dx_v[g, :, 2 * k : 2 * k + 2, :], in_=dx_t[g, k][:])
+        def store_dx(g, pair):
+            nc.sync.dma_start(out=dx_v[g, :, 2 * pair : 2 * pair + 2, :], in_=dx_t[g, pair][:])
 
-        def dw(f, t, g):
+        def dw(f, t, *groups):
+            cols = slice(f * HALF + t * P, f * HALF + (t + 1) * P)
+            for g in groups:
+                for n in range(2):
+                    if g == 0:
+                        tag = "turn" if (f, t) in IN_TURN_BANKS else "dw" + str(n)
+                        bank = psum.tile([P, HALF], F32, tag=tag, name="dw_bank")
+                        dw_acc[f, t, n] = bank
+                    nc.tensor.matmul_mx(
+                        out=dw_acc[f, t, n][:],
+                        lhsT=z_tok_codes[:, g, cols].bitcast(E5M2),
+                        lhsT_scale=z_tok_scales[:, g, cols],
+                        rhs=h_codes[:, g, half(n)].bitcast(E4M3),
+                        rhs_scale=h_scales[:, g, half(n)],
+                        start=(g == 0),
+                        stop=(g == GROUPS - 1),
+                    )
+
+        def out_dw(f, t, stores=1):
+            new = pool.tile([P, INS], F32, tag="result", bufs=4, name="dw_tile")
             for n in range(2):
-                if g == 0:
-                    a = psum.tile([P, HALF], F32, tag="acc" + str(n), name="dw_ps")
-                    acc[f, t, n] = a
-                cols = slice(f * HALF + t * P, f * HALF + (t + 1) * P)
-                nc.tensor.matmul_mx(
-                    out=acc[f, t, n][:],
-                    lhsT=zt_c[:, g, cols].bitcast(E5M2),
-                    lhsT_scale=zt_s[:, g, cols],
-                    rhs=h_c[:, g, half(n)].bitcast(E4M3),
-                    rhs_scale=h_s[:, g, half(n)],
-                    start=(g == 0),
-                    stop=(g == GROUPS - 1),
+                nc.vector.tensor_tensor(
+                    out=new[:, half(n)], in0=dw_acc[f, t, n][:], in1=mask[:, f, t, half(n)], op=MULT
                 )
-
-        def out_dw(f, t):
-            o = pool.tile([P, INS], F32, tag="ost", bufs=4, name="dw_tile")
-            for n in range(2):
-                nc.vector.tensor_tensor(out=o[:, half(n)], in0=acc[f, t, n][:], in1=mask[:, f, t, half(n)], op=MUL)
-            nc.sync.dma_start(out=dw_v[f, :, t, :], in_=o[:])
+                if stores == 2:
+                    nc.sync.dma_start(out=dw_v[f, :, t, half(n)], in_=new[:, half(n)])
+            if stores == 1:
+                nc.sync.dma_start(out=dw_v[f, :, t, :], in_=new[:])
 
         with tc.manual_schedule():
-            load_grad(0, 0)
-            load_mask(1)
-            load_pre(0, 0)
-            load_w(1)
-            gate(0, 0)
-            load_mask(0)
             load_w(0)
-            load_grad(0, 1)
-            mask_w(1, 1)
-            mask_w(1, 0)
-            spread_w(1, 1)
-            spread_dz(0, 0)
-            spread_w(1, 0)
-            load_pre(0, 1)
-            quant_w(1, 1)
-            mask_w(0, 1)
-            turn(0, 0)
+            load_mask(0)
+            load_grad(0, cols=half(0), rows=slice(0, 2))
             mask_w(0, 0)
-            load_h(0)
-            spread_w(0, 1)
-            quant_w(1, 0)
-            quant_tok(0, 0)
-            quant_feat(0, 0)
-            spread_w(0, 0)
-            gate(0, 1)
-            spread_dz(0, 1)
-            load_pre(1)
-            load_grad(1)
-            load_h(1)
-            turn(0, 1)
-            quant_w(0, 1)
-            load_grad(2)
-            load_pre(2)
-            quant_feat(0, 1)
-            quant_tok(0, 1)
+            load_pre(0, cols=half(0), rows=slice(0, 2))
+            mask_w(0, 1)
+            load_grad(0, cols=half(1))
+            spread_w(0, 0, "v")
+            load_pre(0, cols=half(1))
+            gate(0, 0, rows=slice(0, 2))
             quant_w(0, 0)
-            spread_h(0, 1)
-            dx(0, 0, "vv")
+            load_pre(0, cols=half(0), rows=slice(2, 4))
+            load_grad(0, cols=half(0), rows=slice(2, 4))
+            spread_w(0, 1)
+            quant_w(0, 1)
+            load_h(0)
+            gate(0, 1)
+            load_w(1)
+            gate(0, 0, rows=slice(2, 4))
+            spread_dz(0, 1)
+            turn(0, 1)
+            spread_dz(0, 0)
             spread_h(0, 0)
-            load_h(2)
+            quant_tok(0, 0)
+            load_mask(1)
+            turn(0, 0)
             quant_h(0, 0)
+            load_grad(1)
+            quant_feat(0, 0)
+            mask_w(1, 0)
+            spread_h(0, 1)
+            spread_w(1, 0)
+            mask_w(1, 1)
+            quant_feat(0, 1)
+            spread_w(1, 1, "v")
+            quant_w(1, 0)
+            quant_w(1, 1)
+            load_pre(1)
+            dx(0, 0)
+            quant_h(0, 1)
+            load_h(2)
+            quant_tok(0, 1)
             gate(1, 0)
             dx(0, 2)
-            dx(0, 1)
-            dx(0, 3)
             gate(1, 1)
-            load_h(3)
-            turn(1, 0)
-            quant_h(0, 1)
-            load_pre(3)
-            turn(1, 1)
-            quant_feat(1, 0)
-            spread_h(1, 0)
-            spread_dz(1, 0)
-            quant_feat(1, 1)
-            dx(1, 0)
-            quant_tok(1, 0)
-            load_grad(3)
-            dx(1, 1)
-            spread_h(1, 1, "v")
-            gate(2, 1)
-            gate(2, 0)
-            dx(1, 2)
-            quant_h(1, 1)
-            turn(2, 1)
-            spread_dz(2, 0)
-            dw(0, 0, 0)
-            quant_h(1, 0)
-            spread_h(2, 1)
-            turn(2, 0)
-            quant_feat(2, 1)
+            spread_h(2, 1, "v")
             spread_h(2, 0)
-            spread_dz(2, 1)
-            quant_h(2, 1)
-            dw(0, 0, 1)
-            store_dx(0, 0)
-            quant_tok(2, 0)
+            spread_dz(1, 0)
+            load_h(1)
+            turn(1, 0)
+            load_grad(2)
+            dx(0, 3)
+            quant_feat(1, 0)
             dw(0, 1, 0)
-            spread_h(3, 0)
-            dx(1, 3, "vs")
-            dw(0, 1, 1)
+            quant_h(2, 1)
+            turn(1, 1)
+            spread_h(1, 1)
+            dw(0, 0, 0)
+            quant_feat(1, 1)
+            dx(1, 2)
+            spread_h(1, 0)
+            quant_tok(1, 0)
             quant_h(2, 0)
+            load_pre(2)
+            quant_h(1, 1)
+            gate(2, 0)
+            dx(1, 0)
+            gate(2, 1)
+            turn(2, 0)
+            dx(1, 1)
+            load_pre(3)
+            spread_dz(2, 0)
+            load_grad(3)
+            turn(2, 1)
+            quant_h(1, 0)
+            load_h(3)
+            dx(0, 1)
+            dw(0, 1, 1)
             quant_feat(2, 0)
             spread_h(3, 1)
-            dx(2, 0)
-            gate(3, 0)
-            gate(3, 1)
-            dw(0, 0, 2)
+            quant_tok(2, 0)
             store_dx(0, 1)
+            store_dx(0, 0)
+            dw(0, 0, 1)
             dw(0, 1, 2)
+            dx(1, 3)
+            gate(3, 1)
+            turn(3, 1)
+            store_dx(1, 1)
+            quant_feat(2, 1)
+            dw(0, 0, 2)
+            gate(3, 0)
+            dx(2, 2)
+            spread_h(3, 0, "v")
             spread_dz(3, 0)
             turn(3, 0)
-            dx(2, 1)
-            turn(3, 1)
             quant_h(3, 0)
-            quant_tok(3, 0)
-            dx(2, 2)
-            quant_h(3, 1)
-            store_dx(1, 0)
-            dw(0, 0, 3)
-            dw(0, 1, 3)
             dx(2, 3)
-            store_dx(1, 1)
-            store_dx(2, 0)
+            store_dx(1, 0)
             store_dx(2, 1)
+            dw(1, 2, 0)
+            quant_tok(3, 0)
+            dx(2, 0)
+            quant_h(3, 1)
             quant_feat(3, 1)
-            out_dw(0, 0)
-            dw(0, 3, 0)
+            dw(0, 1, 3)
+            dx(2, 1)
             out_dw(0, 1)
-            dw(0, 3, 1)
-            dw(0, 3, 2)
             quant_feat(3, 0)
+            store_dx(2, 0)
+            dw(0, 0, 3)
             dw(0, 2, 0)
-            quant_tok(2, 1)
             spread_dz(1, 1)
-            dw(0, 3, 3)
-            dw(0, 2, 1)
-            dw(0, 2, 2)
-            dw(0, 2, 3)
-            out_dw(0, 3)
+            spread_dz(2, 1)
             quant_tok(1, 1)
-            out_dw(0, 2)
+            out_dw(0, 0)
             dx(3, 2)
+            dw(0, 2, 1, 2)
+            dx(3, 3)
+            dw(0, 2, 3)
+            out_dw(0, 2)
+            quant_tok(2, 1)
+            dx(3, 0)
+            dw(0, 3, 0)
             spread_dz(3, 1)
-            dw(1, 1, 0)
-            quant_tok(3, 1)
-            dw(1, 1, 1)
-            dw(1, 1, 2)
+            dw(1, 2, 1)
             dw(1, 0, 0)
-            dx(3, 3, "sv")
             store_dx(3, 1)
             dw(1, 0, 1)
-            dw(1, 1, 3)
-            out_dw(1, 1)
-            dx(3, 0, "vv")
+            quant_tok(3, 1)
             dw(1, 0, 2)
-            dw(1, 0, 3)
-            out_dw(1, 0)
-            dw(1, 2, 0)
             dx(3, 1, "vv")
-            dw(1, 2, 1)
-            dw(1, 3, 0)
-            dw(1, 2, 2)
+            dw(0, 3, 1)
+            dw(1, 2, 2, 3)
+            dw(0, 3, 2, 3)
             store_dx(3, 0)
-            dw(1, 2, 3)
-            dw(1, 3, 1)
-            dw(1, 3, 2)
-            dw(1, 3, 3)
+            dw(1, 0, 3)
             out_dw(1, 2)
-            out_dw(1, 3)
+            dw(1, 1, 0, 1, 2, 3)
+            out_dw(0, 3)
+            out_dw(1, 0)
+            dw(1, 3, 0, 1)
+            out_dw(1, 1)
+            dw(1, 3, 2, 3)
+            out_dw(1, 3, stores=2)

from contextlib import ExitStack

import concourse.mybir as mybir
from concourse.masks import make_identity

TOKENS, FEATS, INS = 2048, 1024, 1024
FLOPS = 2 * (2 * TOKENS * FEATS * INS)
BYTES = 2 * (TOKENS * INS + 2 * FEATS * INS + TOKENS * FEATS) + 4 * (TOKENS * FEATS + TOKENS * INS + FEATS * INS)

F32 = mybir.dt.float32
BF16 = mybir.dt.bfloat16
U32 = mybir.dt.uint32
U8 = mybir.dt.uint8
E4M3 = mybir.dt.float8_e4m3fn_x4
E5M2 = mybir.dt.float8_e5m2_x4
MULT = mybir.AluOpType.mult
IS_GT = mybir.AluOpType.is_gt

P = 128
PACK = 4
HALF = P * PACK
GROUPS = TOKENS // HALF

IN_TURN_BANKS = ((1, 1), (1, 2))


def tile_scm_mlp_pa_v_kernel(tc, h_in, w, masks, mu, sigma, z, pre, grad_out, out_0, out_1):
    nc = tc.nc
    pre_v = pre.rearrange("(g p j) w -> g p j w", p=P, j=PACK)
    grad_v = grad_out.rearrange("(g p j) w -> g p j w", p=P, j=PACK)
    h_v = h_in.rearrange("(g p j) i -> g p j i", p=P, j=PACK)
    w_v = w[0, :, :].rearrange("(f q t) i -> f q t i", q=P, t=PACK)
    mask_v = masks[0, :, :].rearrange("(f q t) i -> f q t i", q=P, t=PACK)
    dx_v = out_0.rearrange("(g p j) i -> g p j i", p=P, j=PACK)
    dw_v = out_1[0, :, :].rearrange("(f q t) i -> f q t i", q=P, t=PACK)

    def half(n):
        return slice(n * HALF, (n + 1) * HALF)

    with ExitStack() as ctx:
        keep = ctx.enter_context(tc.tile_pool(name="keep", bufs=1))
        pool = ctx.enter_context(tc.tile_pool(name="pool", bufs=2))
        psum = ctx.enter_context(tc.psum_pool(name="psum", bufs=2))

        ident = keep.tile([P, P], F32, name="ident")
        make_identity(nc, ident[:])

        z_tok_codes = keep.tile([P, GROUPS, FEATS], U32, align_bytes=64, name="z_tok_codes")
        z_tok_scales = keep.tile([P, GROUPS, FEATS], U8, align_bytes=64, name="z_tok_scales")
        h_codes = keep.tile([P, GROUPS, INS], U32, align_bytes=64, name="h_codes")
        h_scales = keep.tile([P, GROUPS, INS], U8, align_bytes=64, name="h_scales")
        w_codes = keep.tile([P, 2, INS], U32, align_bytes=64, name="w_codes")
        w_scales = keep.tile([P, 2, INS], U8, align_bytes=64, name="w_scales")
        mask = keep.tile([P, 2, PACK, INS], BF16, align_bytes=64, name="mask")

        pre_t, grad_t, h_t, w_t, dz_t = {}, {}, {}, {}, {}
        dz_tok_by4, dz_feat_by4, h_by4, w_by4 = {}, {}, {}, {}
        z_feat_codes, z_feat_scales = {}, {}
        dx_t, dw_acc = {}, {}

        def move(engine, out, in_):
            if engine == "s":
                nc.scalar.copy(out=out, in_=in_)
            else:
                nc.vector.tensor_copy(out=out, in_=in_)

        def load_step_part(src, tiles, dtype, tag, g, cols, rows):
            if g not in tiles:
                new = pool.tile([P, PACK, FEATS], dtype, tag=tag, name="group_tile")
                tiles[g] = new
            nc.sync.dma_start(out=tiles[g][:, rows, cols], in_=src[g, :, rows, cols])

        def load_pre(g, cols=slice(0, FEATS), rows=slice(0, PACK)):
            load_step_part(pre_v, pre_t, F32, "pre", g, cols, rows)

        def load_grad(g, cols=slice(0, FEATS), rows=slice(0, PACK)):
            load_step_part(grad_v, grad_t, BF16, "grad", g, cols, rows)

        def load_h(g):
            new = pool.tile([P, PACK, INS], BF16, tag="h_or_w", bufs=3, name="h_tile")
            nc.sync.dma_start(out=new[:], in_=h_v[g, :, :, :])
            h_t[g] = new

        def load_w(f):
            new = pool.tile([P, PACK, INS], BF16, tag="h_or_w", bufs=3, name="w_tile")
            nc.sync.dma_start(out=new[:], in_=w_v[f, :, :, :])
            w_t[f] = new

        def load_mask(f):
            nc.sync.dma_start(out=mask[:, f, :, :], in_=mask_v[f, :, :, :])

        def gate(g, f, rows=slice(0, PACK)):
            if (g, f) not in dz_t:
                new = pool.tile([P, PACK, HALF], BF16, tag="dz", bufs=5, align_bytes=64, name="dz_tile")
                dz_t[g, f] = new
            nc.vector.scalar_tensor_tensor(
                out=dz_t[g, f][:, rows, :],
                in0=pre_t[g][:, rows, half(f)],
                scalar=0.0,
                in1=grad_t[g][:, rows, half(f)],
                op0=IS_GT,
                op1=MULT,
            )

        def turn(g, f):
            words = dz_t[g, f][:].rearrange("p j w -> p (j w)").bitcast(F32)
            new = pool.tile([P, PACK, P, PACK], BF16, tag="dz_feat_by4", align_bytes=64, name="feat_tile")
            dz_feat_by4[g, f] = new
            new_words = new[:].rearrange("q j p t -> q (j p t)").bitcast(F32)
            new_words = new_words.rearrange("q (j p u) -> q j p u", j=PACK, u=2)
            for pair in range(2):
                bank = psum.tile([P, 2, 2, P], F32, tag="turn", name="turn_bank")
                for k in range(2):
                    for u in range(2):
                        first = (2 * pair + k) * (HALF // 2) + u
                        nc.tensor.transpose(bank[:, k, u, :], words[:, first : first + HALF // 2 - 1 : 2], ident[:])
                nc.scalar.copy(
                    out=new_words[:, 2 * pair : 2 * pair + 2, :, :], in_=bank[:].rearrange("q k u p -> q k p u")
                )

        def quant_feat(g, f):
            if g not in z_feat_codes:
                codes = pool.tile([P, 2, HALF], U32, tag="z_feat_codes", align_bytes=64, name="feat_codes")
                scales = pool.tile([P, 2, HALF], U8, tag="z_feat_scales", align_bytes=64, name="feat_scales")
                z_feat_codes[g], z_feat_scales[g] = codes, scales
            nc.vector.quantize_mx(
                out=z_feat_codes[g][:, f, :].bitcast(E5M2),
                scales=z_feat_scales[g][:, f, :],
                in_=dz_feat_by4[g, f][:].rearrange("q j p t -> q (j p t)"),
            )

        def spread_dz(g, f):
            new = pool.tile([P, PACK, P, PACK], BF16, tag="dz_tok_by4", align_bytes=64, name="tok_tile")
            nc.vector.tensor_copy(
                out=new[:].rearrange("p t q j -> p q t j"),
                in_=dz_t[g, f][:].rearrange("p j (q t) -> p q t j", t=PACK),
            )
            dz_tok_by4[g, f] = new

        def quant_tok(g, f):
            nc.vector.quantize_mx(
                out=z_tok_codes[:, g, half(f)].bitcast(E5M2),
                scales=z_tok_scales[:, g, half(f)],
                in_=dz_tok_by4[g, f][:].rearrange("p t q j -> p (t q j)"),
            )

        def by4(engine, src):
            new = pool.tile([P, HALF, PACK], BF16, tag="by4", bufs=3, align_bytes=64, name="by4_tile")
            move(engine, new[:].rearrange("p (c i) t -> p c t i", i=4), src.rearrange("p t (c i) -> p c t i", i=4))
            return new

        def spread_h(g, n, engine="s"):
            h_by4[g, n] = by4(engine, h_t[g][:, :, half(n)])

        def quant_h(g, n):
            nc.vector.quantize_mx(
                out=h_codes[:, g, half(n)].bitcast(E4M3),
                scales=h_scales[:, g, half(n)],
                in_=h_by4[g, n][:].rearrange("p i j -> p (i j)"),
            )

        def mask_w(f, n):
            nc.vector.tensor_tensor(
                out=w_t[f][:, :, half(n)], in0=w_t[f][:, :, half(n)], in1=mask[:, f, :, half(n)], op=MULT
            )

        def spread_w(f, n, engine="s"):
            w_by4[f, n] = by4(engine, w_t[f][:, :, half(n)])

        def quant_w(f, n):
            nc.vector.quantize_mx(
                out=w_codes[:, f, half(n)].bitcast(E4M3),
                scales=w_scales[:, f, half(n)],
                in_=w_by4[f, n][:].rearrange("q i t -> q (i t)"),
            )

        def dx(g, j, engines="ss"):
            pair, k = divmod(j, 2)
            if (g, pair) not in dx_t:
                new = pool.tile([P, 2, INS], F32, tag="result", bufs=4, name="dx_tile")
                dx_t[g, pair] = new
            cols = slice(j * P, (j + 1) * P)
            banks = []
            for n in range(2):
                bank = psum.tile([P, HALF], F32, tag="dx", name="dx_bank")
                for f in range(2):
                    nc.tensor.matmul_mx(
                        out=bank[:],
                        lhsT=z_feat_codes[g][:, f, cols].bitcast(E5M2),
                        lhsT_scale=z_feat_scales[g][:, f, cols],
                        rhs=w_codes[:, f, half(n)].bitcast(E4M3),
                        rhs_scale=w_scales[:, f, half(n)],
                        start=(f == 0),
                        stop=(f == 1),
                    )
                banks.append(bank)
            for n in range(2):
                move(engines[n], dx_t[g, pair][:, k, half(n)], banks[n][:])

        def store_dx(g, pair):
            nc.sync.dma_start(out=dx_v[g, :, 2 * pair : 2 * pair + 2, :], in_=dx_t[g, pair][:])

        def dw(f, t, *groups):
            cols = slice(f * HALF + t * P, f * HALF + (t + 1) * P)
            for g in groups:
                for n in range(2):
                    if g == 0:
                        tag = "turn" if (f, t) in IN_TURN_BANKS else "dw" + str(n)
                        bank = psum.tile([P, HALF], F32, tag=tag, name="dw_bank")
                        dw_acc[f, t, n] = bank
                    nc.tensor.matmul_mx(
                        out=dw_acc[f, t, n][:],
                        lhsT=z_tok_codes[:, g, cols].bitcast(E5M2),
                        lhsT_scale=z_tok_scales[:, g, cols],
                        rhs=h_codes[:, g, half(n)].bitcast(E4M3),
                        rhs_scale=h_scales[:, g, half(n)],
                        start=(g == 0),
                        stop=(g == GROUPS - 1),
                    )

        def out_dw(f, t, stores=1):
            new = pool.tile([P, INS], F32, tag="result", bufs=4, name="dw_tile")
            for n in range(2):
                nc.vector.tensor_tensor(
                    out=new[:, half(n)], in0=dw_acc[f, t, n][:], in1=mask[:, f, t, half(n)], op=MULT
                )
                if stores == 2:
                    nc.sync.dma_start(out=dw_v[f, :, t, half(n)], in_=new[:, half(n)])
            if stores == 1:
                nc.sync.dma_start(out=dw_v[f, :, t, :], in_=new[:])

        with tc.manual_schedule():
            load_w(0)
            load_mask(0)
            load_grad(0, cols=half(0), rows=slice(0, 2))
            mask_w(0, 0)
            load_pre(0, cols=half(0), rows=slice(0, 2))
            mask_w(0, 1)
            load_grad(0, cols=half(1))
            spread_w(0, 0, "v")
            load_pre(0, cols=half(1))
            gate(0, 0, rows=slice(0, 2))
            quant_w(0, 0)
            load_pre(0, cols=half(0), rows=slice(2, 4))
            load_grad(0, cols=half(0), rows=slice(2, 4))
            spread_w(0, 1)
            quant_w(0, 1)
            load_h(0)
            gate(0, 1)
            load_w(1)
            gate(0, 0, rows=slice(2, 4))
            spread_dz(0, 1)
            turn(0, 1)
            spread_dz(0, 0)
            spread_h(0, 0)
            quant_tok(0, 0)
            load_mask(1)
            turn(0, 0)
            quant_h(0, 0)
            load_grad(1)
            quant_feat(0, 0)
            mask_w(1, 0)
            spread_h(0, 1)
            spread_w(1, 0)
            mask_w(1, 1)
            quant_feat(0, 1)
            spread_w(1, 1, "v")
            quant_w(1, 0)
            quant_w(1, 1)
            load_pre(1)
            dx(0, 0)
            quant_h(0, 1)
            load_h(2)
            quant_tok(0, 1)
            gate(1, 0)
            dx(0, 2)
            gate(1, 1)
            spread_h(2, 1, "v")
            spread_h(2, 0)
            spread_dz(1, 0)
            load_h(1)
            turn(1, 0)
            load_grad(2)
            dx(0, 3)
            quant_feat(1, 0)
            dw(0, 1, 0)
            quant_h(2, 1)
            turn(1, 1)
            spread_h(1, 1)
            dw(0, 0, 0)
            quant_feat(1, 1)
            dx(1, 2)
            spread_h(1, 0)
            quant_tok(1, 0)
            quant_h(2, 0)
            load_pre(2)
            quant_h(1, 1)
            gate(2, 0)
            dx(1, 0)
            gate(2, 1)
            turn(2, 0)
            dx(1, 1)
            load_pre(3)
            spread_dz(2, 0)
            load_grad(3)
            turn(2, 1)
            quant_h(1, 0)
            load_h(3)
            dx(0, 1)
            dw(0, 1, 1)
            quant_feat(2, 0)
            spread_h(3, 1)
            quant_tok(2, 0)
            store_dx(0, 1)
            store_dx(0, 0)
            dw(0, 0, 1)
            dw(0, 1, 2)
            dx(1, 3)
            gate(3, 1)
            turn(3, 1)
            store_dx(1, 1)
            quant_feat(2, 1)
            dw(0, 0, 2)
            gate(3, 0)
            dx(2, 2)
            spread_h(3, 0, "v")
            spread_dz(3, 0)
            turn(3, 0)
            quant_h(3, 0)
            dx(2, 3)
            store_dx(1, 0)
            store_dx(2, 1)
            dw(1, 2, 0)
            quant_tok(3, 0)
            dx(2, 0)
            quant_h(3, 1)
            quant_feat(3, 1)
            dw(0, 1, 3)
            dx(2, 1)
            out_dw(0, 1)
            quant_feat(3, 0)
            store_dx(2, 0)
            dw(0, 0, 3)
            dw(0, 2, 0)
            spread_dz(1, 1)
            spread_dz(2, 1)
            quant_tok(1, 1)
            out_dw(0, 0)
            dx(3, 2)
            dw(0, 2, 1, 2)
            dx(3, 3)
            dw(0, 2, 3)
            out_dw(0, 2)
            quant_tok(2, 1)
            dx(3, 0)
            dw(0, 3, 0)
            spread_dz(3, 1)
            dw(1, 2, 1)
            dw(1, 0, 0)
            store_dx(3, 1)
            dw(1, 0, 1)
            quant_tok(3, 1)
            dw(1, 0, 2)
            dx(3, 1, "vv")
            dw(0, 3, 1)
            dw(1, 2, 2, 3)
            dw(0, 3, 2, 3)
            store_dx(3, 0)
            dw(1, 0, 3)
            out_dw(1, 2)
            dw(1, 1, 0, 1, 2, 3)
            out_dw(0, 3)
            out_dw(1, 0)
            dw(1, 3, 0, 1)
            out_dw(1, 1)
            dw(1, 3, 2, 3)
            out_dw(1, 3, stores=2)
